import numpy as np
import ml_dtypes


def mxq(x, axis, fmt="e4m3"):
    dtype, down = {"e4m3": (ml_dtypes.float8_e4m3fn, 7), "e5m2": (ml_dtypes.float8_e5m2, 14)}[fmt]
    v = np.moveaxis(np.asarray(x, np.float32).astype(ml_dtypes.bfloat16).astype(np.float64), axis, -1)
    blocks = v.reshape(v.shape[:-1] + (-1, 32))
    amax = np.abs(blocks).max(-1, keepdims=True)
    byte = np.maximum(np.where(amax > 0, np.frexp(amax)[1] - 1 + 127, 0) - down, 1)
    scale = np.exp2(byte - 127.0)
    codes = (blocks / scale).astype(np.float32).astype(dtype).astype(np.float64)
    return np.moveaxis((codes * scale).reshape(v.shape), -1, axis)


WIDE = False


def mx_kscale(k):
    if not WIDE:
        return np.ones(k)
    levels = np.array([20, -20, 10, -10, 0])
    a = np.random.permutation(np.resize(levels, k // 512 * 4)).reshape(k // 512, 4)
    idx = np.arange(k)
    return np.exp2(a[idx // 512, idx % 128 // 32])


BF16 = ml_dtypes.bfloat16


def bf(x):
    return np.asarray(x, np.float32).astype(BF16)


def f64(x):
    return np.asarray(x).astype(np.float64)


B, P, D = 4096, 2, 512
IN = P * D


def sigmoid(v):
    return 1.0 / (1.0 + np.exp(-v))


def setup_inputs():
    s = mx_kscale(B)[:, None]
    x0 = bf(np.random.standard_normal((B, IN)))
    weights = bf(np.random.standard_normal((P, D, D)) / np.sqrt(D))
    bias = bf(np.random.standard_normal(IN) * 0.3)
    gain = bf(1.3 + 0.1 * np.random.standard_normal(1))
    nb0 = bf(0.3 + 0.05 * np.random.standard_normal(1))
    gamma = bf(0.5 + 0.3 * np.random.standard_normal(IN))
    beta = bf(np.random.standard_normal(IN))
    g = bf(np.random.standard_normal((B, IN)) * np.exp2(np.random.randint(-12, 1, (B, 1))) / s)
    xn0 = (f64(x0) * f64(gain) + f64(nb0)).reshape(B, P, D).transpose(1, 0, 2)
    y = (xn0 @ f64(weights)).transpose(1, 0, 2).reshape(B, IN) + f64(bias)
    return {"x": bf(f64(x0) * s), "weights": weights, "bias": bias, "gain": gain,
            "norm_bias": bf(f64(nb0) * s.min()), "gamma": gamma, "beta": beta,
            "y": np.asarray(y, np.float32), "grad_out": g}


def reference(x, weights, bias, gain, norm_bias, gamma, beta, y, grad_out):
    gm, bt, yf = f64(gamma), f64(beta), f64(y)
    x_norm = f64(x) * f64(gain) + f64(norm_bias)
    sg = sigmoid(bt * yf)
    dy = f64(grad_out) * (gm + (1.0 - gm) * sg * (1.0 + bt * yf * (1.0 - sg)))
    xp = x_norm.reshape(B, P, D).transpose(1, 0, 2)
    dp = dy.reshape(B, P, D).transpose(1, 0, 2)
    return mxq(xp, 1, "e4m3").transpose(0, 2, 1) @ mxq(dp, 1, "e5m2")

@@ -1,0 +1,280 @@
+from contextlib import ExitStack
+
+import concourse.mybir as mybir
+from concourse.masks import make_identity
+
+F32 = mybir.dt.float32
+BF16 = mybir.dt.bfloat16
+U32 = mybir.dt.uint32
+U8 = mybir.dt.uint8
+E4M3_X4 = mybir.dt.float8_e4m3fn_x4
+E5M2_X4 = mybir.dt.float8_e5m2_x4
+FUNC = mybir.ActivationFunctionType
+ALU = mybir.AluOpType
+
+P = 128
+PACK = 4
+K_PASS = P * PACK
+TOKENS = 4096
+PARTS = 2
+D = 512
+PASSES = TOKENS // K_PASS
+BLOCKS = D // P
+VEC_ROWS = PARTS * BLOCKS
+ROUNDS = PARTS * PASSES
+UNITS = ROUNDS * BLOCKS
+
+Y_LEAD = 2
+X_LEAD = BLOCKS
+BACK_LAG = 1
+FINISH_LAG = 2
+MULTIPLY_LAG = 3
+STORE_LAG = 5
+LOAD_LEAD = 2
+
+FLOPS = 2 * PARTS * TOKENS * D * D
+
+
+def tile_better_transformer_t_v_kernel(
+    tc, x, weights, bias, gain, norm_bias, gamma, beta, y, grad_out, out
+):
+    nc = tc.nc
+    x_view = x.rearrange("(c p j) f -> c p j f", p=P, j=PACK)
+    y_view = y.rearrange("(c p j) f -> c p j f", p=P, j=PACK)
+    g_view = grad_out.rearrange("(c p j) f -> c p j f", p=P, j=PACK)
+
+    with ExitStack() as ctx:
+        consts = ctx.enter_context(tc.tile_pool(name="consts", bufs=1))
+        loads = ctx.enter_context(tc.tile_pool(name="loads", bufs=3))
+        work = ctx.enter_context(tc.tile_pool(name="work", bufs=3))
+        grouped = ctx.enter_context(tc.tile_pool(name="grouped", bufs=3))
+        quant = ctx.enter_context(tc.tile_pool(name="quant", bufs=3))
+        results = ctx.enter_context(tc.tile_pool(name="results", bufs=BLOCKS))
+        acc_pool = ctx.enter_context(tc.psum_pool(name="acc", bufs=1))
+        to_features = ctx.enter_context(tc.psum_pool(name="to_features", bufs=2))
+        to_tokens = ctx.enter_context(tc.psum_pool(name="to_tokens", bufs=2))
+        ctx.enter_context(tc.manual_schedule())
+
+        x_raw, y_raw, g_raw = {}, {}, {}
+        x_grouped, x_codes, x_scales = {}, {}, {}
+        dy_grouped, dy_codes, dy_scales = {}, {}, {}
+        y_t, tanh_half, silu, damped, corr, corr_t = {}, {}, {}, {}, {}, {}
+        acc = {}
+
+        def round_of(u):
+            return u // BLOCKS
+
+        def starts_round(u):
+            return u % BLOCKS == 0
+
+        def block_cols(u):
+            b = u % BLOCKS
+            return slice(b * P, (b + 1) * P)
+
+        def const_col(u):
+            col = u // (PASSES * BLOCKS) * BLOCKS + u % BLOCKS
+            return slice(col, col + 1)
+
+        def load_round(r):
+            part, c = divmod(r, PASSES)
+            first = part * D
+            x_raw[r] = loads.tile([P, PACK, D], BF16, name="x_raw")
+            nc.sync.dma_start(out=x_raw[r][:], in_=x_view[c, :, :, first : first + D])
+            width = P if r == 0 else D
+            y_raw[r] = loads.tile([P, PACK, D], F32, name="y_raw")
+            for lo in range(0, D, width):
+                nc.sync.dma_start(
+                    out=y_raw[r][:, :, lo : lo + width],
+                    in_=y_view[c, :, :, first + lo : first + lo + width],
+                )
+            g_raw[r] = loads.tile([P, PACK, D], BF16, name="g_raw", bufs=4)
+            nc.sync.dma_start(out=g_raw[r][:], in_=g_view[c, :, :, first : first + D])
+
+        def x_norm_block(u):
+            r = round_of(u)
+            if starts_round(u):
+                x_grouped[r] = grouped.tile([P, D, PACK], BF16, name="x_grouped", align_bytes=64)
+            f_cols = block_cols(u)
+            nc.scalar.activation(
+                out=x_grouped[r][:, f_cols, :].rearrange("p (n i) j -> p n j i", i=4),
+                in_=x_raw[r][:, :, f_cols].rearrange("p j (n i) -> p n j i", i=4),
+                func=FUNC.Identity,
+                bias=shift_col[:, 0:1],
+                scale=gain_col[:, 0:1],
+            )
+
+        def quantise_x(r):
+            x_codes[r] = quant.tile([P, D], U32, name="x_codes", align_bytes=64)
+            x_scales[r] = quant.tile([P, D], U8, name="x_scales", align_bytes=64)
+            nc.vector.quantize_mx(
+                out=x_codes[r][:].bitcast(E4M3_X4),
+                scales=x_scales[r][:],
+                in_=x_grouped[r][:].rearrange("p w j -> p (w j)"),
+            )
+
+        def y_to_features(u):
+            y_t[u] = to_features.tile([P, PACK, P], F32, name="y_t")
+            for j in range(PACK):
+                nc.tensor.transpose(y_t[u][:, j, :], y_raw[round_of(u)][:, j, block_cols(u)], ident[:])
+
+        def activations(u):
+            tanh_half[u] = work.tile([P, PACK, P], F32, name="tanh_half")
+            nc.scalar.activation(
+                out=tanh_half[u][:], in_=y_t[u][:], func=FUNC.Tanh,
+                scale=half_beta_col[:, const_col(u)],
+            )
+            silu[u] = work.tile([P, PACK, P], F32, name="silu")
+            nc.scalar.activation(
+                out=silu[u][:], in_=y_t[u][:], func=FUNC.Silu,
+                scale=beta_col[:, const_col(u)],
+            )
+
+        def damp(u):
+            damped[u] = work.tile([P, PACK, P], F32, name="damped")
+            nc.vector.tensor_scalar(
+                out=damped[u][:], in0=tanh_half[u][:],
+                scalar1=1.0, scalar2=damp_col[:, const_col(u)],
+                op0=ALU.subtract, op1=ALU.mult,
+            )
+
+        def correct(u):
+            corr[u] = work.tile([P, PACK, P], F32, name="corr")
+            nc.vector.scalar_tensor_tensor(
+                out=corr[u][:], in0=silu[u][:], scalar=1.0, in1=damped[u][:],
+                op0=ALU.subtract, op1=ALU.mult,
+            )
+
+        def corr_to_tokens(u):
+            corr_t[u] = to_tokens.tile([P, PACK, P], F32, name="corr_t")
+            for j in range(PACK):
+                nc.tensor.transpose(corr_t[u][:, j, :], corr[u][:, j, :], ident[:])
+
+        def finish_dy(u):
+            r = round_of(u)
+            if starts_round(u):
+                dy_grouped[r] = grouped.tile([P, D, PACK], BF16, name="dy_grouped", align_bytes=64)
+            f_cols = block_cols(u)
+            nc.vector.scalar_tensor_tensor(
+                out=dy_grouped[r][:, f_cols, :],
+                in0=corr_t[u][:].rearrange("p j f -> p f j"),
+                scalar=1.0,
+                in1=g_raw[r][:, :, f_cols].rearrange("p j f -> p f j"),
+                op0=ALU.add, op1=ALU.mult,
+            )
+
+        def quantise_dy(r):
+            dy_codes[r] = quant.tile([P, D], U32, name="dy_codes", align_bytes=64)
+            dy_scales[r] = quant.tile([P, D], U8, name="dy_scales", align_bytes=64)
+            nc.vector.quantize_mx(
+                out=dy_codes[r][:].bitcast(E5M2_X4),
+                scales=dy_scales[r][:],
+                in_=dy_grouped[r][:].rearrange("p w j -> p (w j)"),
+            )
+
+        def multiply(r):
+            part, c = divmod(r, PASSES)
+            if c == 0:
+                acc[part] = [acc_pool.tile([P, D], F32, name="acc%d" % i) for i in range(BLOCKS)]
+            for i in range(BLOCKS):
+                i_cols = slice(i * P, (i + 1) * P)
+                nc.tensor.matmul_mx(
+                    out=acc[part][i][:],
+                    lhsT=x_codes[r][:, i_cols].bitcast(E4M3_X4),
+                    lhsT_scale=x_scales[r][:, i_cols],
+                    rhs=dy_codes[r][:].bitcast(E5M2_X4),
+                    rhs_scale=dy_scales[r][:],
+                    start=(c == 0),
+                    stop=(c == PASSES - 1),
+                )
+
+        def store_part(part):
+            for i in range(BLOCKS):
+                result = results.tile([P, D], F32, name="result")
+                if i % 2 == 0:
+                    nc.vector.tensor_copy(out=result[:], in_=acc[part][i][:])
+                else:
+                    nc.scalar.copy(out=result[:], in_=acc[part][i][:])
+                nc.sync.dma_start(out=out[part, i * P : (i + 1) * P, :], in_=result[:])
+
+        table_in = consts.tile([P, 1], F32)
+        nc.vector.memset(table_in[:], 0.0)
+        table_out = consts.tile([P, 1], F32)
+        nc.scalar.activation(out=table_out[:], in_=table_in[:], func=FUNC.Silu)
+
+        ident = consts.tile([P, P], F32)
+        make_identity(nc, ident[:])
+
+        gain_bf = consts.tile([P, 1], BF16)
+        nc.sync.dma_start(out=gain_bf[:], in_=gain.partition_broadcast(P))
+        shift_bf = consts.tile([P, 1], BF16)
+        nc.sync.dma_start(out=shift_bf[:], in_=norm_bias.partition_broadcast(P))
+        vec_bf = consts.tile([2 * VEC_ROWS, P], BF16)
+        nc.sync.dma_start(out=vec_bf[0:VEC_ROWS, :], in_=beta.rearrange("(r f) -> r f", f=P))
+        nc.sync.dma_start(
+            out=vec_bf[VEC_ROWS : 2 * VEC_ROWS, :], in_=gamma.rearrange("(r f) -> r f", f=P)
+        )
+        for r in range(LOAD_LEAD):
+            load_round(r)
+
+        gain_col = consts.tile([P, 1], F32)
+        nc.vector.tensor_copy(out=gain_col[:], in_=gain_bf[:])
+        shift_col = consts.tile([P, 1], F32)
+        nc.vector.tensor_copy(out=shift_col[:], in_=shift_bf[:])
+        vec_rows = consts.tile([P, P], F32)
+        nc.vector.memset(vec_rows[:], 0.0)
+        nc.vector.tensor_copy(out=vec_rows[0 : 2 * VEC_ROWS, :], in_=vec_bf[:])
+        vec_cols = to_features.tile([P, P], F32, tag="y_t")
+        nc.tensor.transpose(vec_cols[:], vec_rows[:], ident[:])
+        beta_col = consts.tile([P, VEC_ROWS], F32)
+        nc.vector.tensor_copy(out=beta_col[:], in_=vec_cols[:, 0:VEC_ROWS])
+        half_beta_col = consts.tile([P, VEC_ROWS], F32)
+        nc.vector.tensor_scalar_mul(out=half_beta_col[:], in0=vec_cols[:, 0:VEC_ROWS], scalar1=0.5)
+        damp_col = consts.tile([P, VEC_ROWS], F32)
+        nc.vector.tensor_scalar(
+            out=damp_col[:], in0=vec_cols[:, VEC_ROWS : 2 * VEC_ROWS],
+            scalar1=1.0, scalar2=0.5, op0=ALU.subtract, op1=ALU.mult,
+        )
+
+        def is_unit(u):
+            return 0 <= u < UNITS
+
+        def round_ending_at(u):
+            return round_of(u) if is_unit(u) and starts_round(u + 1) else None
+
+        for u in range(X_LEAD):
+            x_norm_block(u)
+        for u in range(Y_LEAD):
+            y_to_features(u)
+
+        for s in range(UNITS + STORE_LAG + 1):
+            if starts_round(s) and round_of(s) + LOAD_LEAD < ROUNDS:
+                load_round(round_of(s) + LOAD_LEAD)
+
+            if is_unit(s):
+                activations(s)
+            if is_unit(s + X_LEAD):
+                x_norm_block(s + X_LEAD)
+
+            if is_unit(s):
+                damp(s)
+            full_round = round_ending_at(s - MULTIPLY_LAG)
+            if full_round is not None:
+                quantise_dy(full_round)
+            if is_unit(s - FINISH_LAG):
+                finish_dy(s - FINISH_LAG)
+            x_round = round_ending_at(s + X_LEAD - 1)
+            if x_round is not None:
+                quantise_x(x_round)
+            if is_unit(s):
+                correct(s)
+
+            if is_unit(s - BACK_LAG):
+                corr_to_tokens(s - BACK_LAG)
+            if is_unit(s + Y_LEAD):
+                y_to_features(s + Y_LEAD)
+            if full_round is not None:
+                multiply(full_round)
+
+            stored_round = round_ending_at(s - STORE_LAG)
+            if stored_round is not None and (stored_round + 1) % PASSES == 0:
+                store_part(stored_round // PASSES)

@@ -29,7 +29,8 @@ X_LEAD = BLOCKS
 BACK_LAG = 1
 FINISH_LAG = 2
 MULTIPLY_LAG = 3
-STORE_LAG = 5
+PASSES_A_STEP = 2
+STORE_LAG = 6
 LOAD_LEAD = 2
 
 FLOPS = 2 * PARTS * TOKENS * D * D
@@ -171,11 +172,11 @@ def tile_better_transformer_t_v_kernel(
                 in_=dy_grouped[r][:].rearrange("p w j -> p (w j)"),
             )
 
-        def multiply(r):
+        def multiply(r, first_block):
             part, c = divmod(r, PASSES)
-            if c == 0:
+            if c == 0 and first_block == 0:
                 acc[part] = [acc_pool.tile([P, D], F32, name="acc%d" % i) for i in range(BLOCKS)]
-            for i in range(BLOCKS):
+            for i in range(first_block, first_block + PASSES_A_STEP):
                 i_cols = slice(i * P, (i + 1) * P)
                 nc.tensor.matmul_mx(
                     out=acc[part][i][:],
@@ -272,8 +273,10 @@ def tile_better_transformer_t_v_kernel(
                 corr_to_tokens(s - BACK_LAG)
             if is_unit(s + Y_LEAD):
                 y_to_features(s + Y_LEAD)
-            if full_round is not None:
-                multiply(full_round)
+            for first_block in range(0, BLOCKS, PASSES_A_STEP):
+                ready_round = round_ending_at(s - MULTIPLY_LAG - first_block // PASSES_A_STEP)
+                if ready_round is not None:
+                    multiply(ready_round, first_block)
 
             stored_round = round_ending_at(s - STORE_LAG)
             if stored_round is not None and (stored_round + 1) % PASSES == 0:

@@ -29,8 +29,8 @@ X_LEAD = BLOCKS
 BACK_LAG = 1
 FINISH_LAG = 2
 MULTIPLY_LAG = 3
-PASSES_A_STEP = 2
-STORE_LAG = 6
+PASSES_A_STEP = 1
+STORE_LAG = 7
 LOAD_LEAD = 2
 
 FLOPS = 2 * PARTS * TOKENS * D * D
@@ -269,6 +269,10 @@ def tile_better_transformer_t_v_kernel(
             if is_unit(s):
                 correct(s)
 
+            stored_round = round_ending_at(s - STORE_LAG)
+            if stored_round is not None and (stored_round + 1) % PASSES == 0:
+                store_part(stored_round // PASSES)
+
             if is_unit(s - BACK_LAG):
                 corr_to_tokens(s - BACK_LAG)
             if is_unit(s + Y_LEAD):
@@ -277,7 +281,3 @@ def tile_better_transformer_t_v_kernel(
                 ready_round = round_ending_at(s - MULTIPLY_LAG - first_block // PASSES_A_STEP)
                 if ready_round is not None:
                     multiply(ready_round, first_block)
-
-            stored_round = round_ending_at(s - STORE_LAG)
-            if stored_round is not None and (stored_round + 1) % PASSES == 0:
-                store_part(stored_round // PASSES)

@@ -26,11 +26,12 @@ UNITS = ROUNDS * BLOCKS
 
 Y_LEAD = 2
 X_LEAD = BLOCKS
-BACK_LAG = 1
-FINISH_LAG = 2
-MULTIPLY_LAG = 3
+CORRECT_LAG = 1
+BACK_LAG = 2
+FINISH_LAG = 3
+MULTIPLY_LAG = 4
 PASSES_A_STEP = 1
-STORE_LAG = 7
+STORE_LAG = 8
 LOAD_LEAD = 2
 
 FLOPS = 2 * PARTS * TOKENS * D * D
@@ -61,6 +62,12 @@ def tile_better_transformer_t_v_kernel(
         dy_grouped, dy_codes, dy_scales = {}, {}, {}
         y_t, tanh_half, silu, damped, corr, corr_t = {}, {}, {}, {}, {}, {}
         acc = {}
+
+        def damp_on_scalar(u):
+            return True
+
+        def x_on_vector(u):
+            return True
 
         def round_of(u):
             return u // BLOCKS
@@ -96,6 +103,14 @@ def tile_better_transformer_t_v_kernel(
             if starts_round(u):
                 x_grouped[r] = grouped.tile([P, D, PACK], BF16, name="x_grouped", align_bytes=64)
             f_cols = block_cols(u)
+            if x_on_vector(u):
+                nc.vector.tensor_scalar(
+                    out=x_grouped[r][:, f_cols, :].rearrange("p (n i) j -> p n j i", i=4),
+                    in0=x_raw[r][:, :, f_cols].rearrange("p j (n i) -> p n j i", i=4),
+                    scalar1=gain_col[:, 0:1], scalar2=shift_col[:, 0:1],
+                    op0=ALU.mult, op1=ALU.add,
+                )
+                return
             nc.scalar.activation(
                 out=x_grouped[r][:, f_cols, :].rearrange("p (n i) j -> p n j i", i=4),
                 in_=x_raw[r][:, :, f_cols].rearrange("p j (n i) -> p n j i", i=4),
@@ -132,6 +147,12 @@ def tile_better_transformer_t_v_kernel(
 
         def damp(u):
             damped[u] = work.tile([P, PACK, P], F32, name="damped")
+            if damp_on_scalar(u):
+                nc.scalar.activation(
+                    out=damped[u][:], in_=tanh_half[u][:], func=FUNC.Identity,
+                    scale=damp_col[:, const_col(u)], bias=neg_damp_col[:, const_col(u)],
+                )
+                return
             nc.vector.tensor_scalar(
                 out=damped[u][:], in0=tanh_half[u][:],
                 scalar1=1.0, scalar2=damp_col[:, const_col(u)],
@@ -236,6 +257,12 @@ def tile_better_transformer_t_v_kernel(
             scalar1=1.0, scalar2=0.5, op0=ALU.subtract, op1=ALU.mult,
         )
 
+        neg_damp_col = consts.tile([P, VEC_ROWS], F32)
+        nc.vector.tensor_scalar(
+            out=neg_damp_col[:], in0=vec_cols[:, VEC_ROWS : 2 * VEC_ROWS],
+            scalar1=-0.5, scalar2=0.5, op0=ALU.mult, op1=ALU.add,
+        )
+
         def is_unit(u):
             return 0 <= u < UNITS
 
@@ -253,10 +280,12 @@ def tile_better_transformer_t_v_kernel(
 
             if is_unit(s):
                 activations(s)
-            if is_unit(s + X_LEAD):
+                if damp_on_scalar(s):
+                    damp(s)
+            if is_unit(s + X_LEAD) and not x_on_vector(s + X_LEAD):
                 x_norm_block(s + X_LEAD)
 
-            if is_unit(s):
+            if is_unit(s) and not damp_on_scalar(s):
                 damp(s)
             full_round = round_ending_at(s - MULTIPLY_LAG)
             if full_round is not None:
@@ -266,8 +295,10 @@ def tile_better_transformer_t_v_kernel(
             x_round = round_ending_at(s + X_LEAD - 1)
             if x_round is not None:
                 quantise_x(x_round)
-            if is_unit(s):
-                correct(s)
+            if is_unit(s - CORRECT_LAG):
+                correct(s - CORRECT_LAG)
+            if is_unit(s + X_LEAD) and x_on_vector(s + X_LEAD):
+                x_norm_block(s + X_LEAD)
 
             stored_round = round_ending_at(s - STORE_LAG)
             if stored_round is not None and (stored_round + 1) % PASSES == 0:

@@ -83,20 +83,24 @@ def tile_better_transformer_t_v_kernel(
             col = u // (PASSES * BLOCKS) * BLOCKS + u % BLOCKS
             return slice(col, col + 1)
 
-        def load_round(r):
+        def load_x(r):
             part, c = divmod(r, PASSES)
-            first = part * D
-            x_raw[r] = loads.tile([P, PACK, D], BF16, name="x_raw")
-            nc.sync.dma_start(out=x_raw[r][:], in_=x_view[c, :, :, first : first + D])
-            width = P if r == 0 else D
-            y_raw[r] = loads.tile([P, PACK, D], F32, name="y_raw")
-            for lo in range(0, D, width):
-                nc.sync.dma_start(
-                    out=y_raw[r][:, :, lo : lo + width],
-                    in_=y_view[c, :, :, first + lo : first + lo + width],
-                )
+            x_raw[r] = loads.tile([P, PACK, D], BF16, name="x_raw", bufs=4)
+            nc.sync.dma_start(out=x_raw[r][:], in_=x_view[c, :, :, part * D : (part + 1) * D])
+
+        def load_y(r, lo, width):
+            part, c = divmod(r, PASSES)
+            if lo == 0:
+                y_raw[r] = loads.tile([P, PACK, D], F32, name="y_raw")
+            nc.sync.dma_start(
+                out=y_raw[r][:, :, lo : lo + width],
+                in_=y_view[c, :, :, part * D + lo : part * D + lo + width],
+            )
+
+        def load_g(r):
+            part, c = divmod(r, PASSES)
             g_raw[r] = loads.tile([P, PACK, D], BF16, name="g_raw", bufs=4)
-            nc.sync.dma_start(out=g_raw[r][:], in_=g_view[c, :, :, first : first + D])
+            nc.sync.dma_start(out=g_raw[r][:], in_=g_view[c, :, :, part * D : (part + 1) * D])
 
         def x_norm_block(u):
             r = round_of(u)
@@ -212,7 +216,7 @@ def tile_better_transformer_t_v_kernel(
         def store_part(part):
             for i in range(BLOCKS):
                 result = results.tile([P, D], F32, name="result")
-                if i % 2 == 0:
+                if i % 2 == 0 and part == PARTS - 1:
                     nc.vector.tensor_copy(out=result[:], in_=acc[part][i][:])
                 else:
                     nc.scalar.copy(out=result[:], in_=acc[part][i][:])
@@ -235,8 +239,19 @@ def tile_better_transformer_t_v_kernel(
         nc.sync.dma_start(
             out=vec_bf[VEC_ROWS : 2 * VEC_ROWS, :], in_=gamma.rearrange("(r f) -> r f", f=P)
         )
-        for r in range(LOAD_LEAD):
-            load_round(r)
+        load_y(0, 0, P)
+        load_x(0)
+        load_y(0, P, P)
+        load_x(1)
+        load_y(0, 2 * P, P)
+        load_y(0, 3 * P, P)
+        load_g(0)
+        load_y(1, 0, P)
+        load_y(1, P, P)
+        load_x(2)
+        load_y(1, 2 * P, P)
+        load_y(1, 3 * P, P)
+        load_g(1)
 
         gain_col = consts.tile([P, 1], F32)
         nc.vector.tensor_copy(out=gain_col[:], in_=gain_bf[:])
@@ -275,8 +290,13 @@ def tile_better_transformer_t_v_kernel(
             y_to_features(u)
 
         for s in range(UNITS + STORE_LAG + 1):
-            if starts_round(s) and round_of(s) + LOAD_LEAD < ROUNDS:
-                load_round(round_of(s) + LOAD_LEAD)
+            if starts_round(s):
+                if round_of(s) + LOAD_LEAD < ROUNDS:
+                    load_y(round_of(s) + LOAD_LEAD, 0, D)
+                if round_of(s) + LOAD_LEAD + 1 < ROUNDS:
+                    load_x(round_of(s) + LOAD_LEAD + 1)
+                if round_of(s) + LOAD_LEAD < ROUNDS:
+                    load_g(round_of(s) + LOAD_LEAD)
 
             if is_unit(s):
                 activations(s)

@@ -26,6 +26,8 @@ UNITS = ROUNDS * BLOCKS
 
 Y_LEAD = 2
 X_LEAD = BLOCKS
+DAMP_SCALAR_COLS = 256
+X_SCALAR_EVERY = 3
 CORRECT_LAG = 1
 BACK_LAG = 2
 FINISH_LAG = 3
@@ -67,7 +69,7 @@ def tile_better_transformer_t_v_kernel(
             return True
 
         def x_on_vector(u):
-            return True
+            return u % X_SCALAR_EVERY != X_SCALAR_EVERY - 1
 
         def round_of(u):
             return u // BLOCKS
@@ -152,8 +154,16 @@ def tile_better_transformer_t_v_kernel(
         def damp(u):
             damped[u] = work.tile([P, PACK, P], F32, name="damped")
             if damp_on_scalar(u):
+                damped_flat = damped[u][:].rearrange("p j f -> p (j f)")
+                tanh_flat = tanh_half[u][:].rearrange("p j f -> p (j f)")
+                nc.gpsimd.tensor_scalar(
+                    out=damped_flat[:, DAMP_SCALAR_COLS:], in0=tanh_flat[:, DAMP_SCALAR_COLS:],
+                    scalar1=damp_col[:, const_col(u)], scalar2=neg_damp_col[:, const_col(u)],
+                    op0=ALU.mult, op1=ALU.add,
+                )
                 nc.scalar.activation(
-                    out=damped[u][:], in_=tanh_half[u][:], func=FUNC.Identity,
+                    out=damped_flat[:, 0:DAMP_SCALAR_COLS], in_=tanh_flat[:, 0:DAMP_SCALAR_COLS],
+                    func=FUNC.Identity,
                     scale=damp_col[:, const_col(u)], bias=neg_damp_col[:, const_col(u)],
                 )
                 return
@@ -307,18 +317,18 @@ def tile_better_transformer_t_v_kernel(
 
             if is_unit(s) and not damp_on_scalar(s):
                 damp(s)
-            full_round = round_ending_at(s - MULTIPLY_LAG)
-            if full_round is not None:
-                quantise_dy(full_round)
+            if is_unit(s - CORRECT_LAG):
+                correct(s - CORRECT_LAG)
             if is_unit(s - FINISH_LAG):
                 finish_dy(s - FINISH_LAG)
+            if is_unit(s + X_LEAD) and x_on_vector(s + X_LEAD):
+                x_norm_block(s + X_LEAD)
             x_round = round_ending_at(s + X_LEAD - 1)
             if x_round is not None:
                 quantise_x(x_round)
-            if is_unit(s - CORRECT_LAG):
-                correct(s - CORRECT_LAG)
-            if is_unit(s + X_LEAD) and x_on_vector(s + X_LEAD):
-                x_norm_block(s + X_LEAD)
+            full_round = round_ending_at(s - MULTIPLY_LAG)
+            if full_round is not None:
+                quantise_dy(full_round)
 
             stored_round = round_ending_at(s - STORE_LAG)
             if stored_round is not None and (stored_round + 1) % PASSES == 0:

@@ -125,13 +125,16 @@ def tile_better_transformer_t_v_kernel(
                 scale=gain_col[:, 0:1],
             )
 
-        def quantise_x(r):
-            x_codes[r] = quant.tile([P, D], U32, name="x_codes", align_bytes=64)
-            x_scales[r] = quant.tile([P, D], U8, name="x_scales", align_bytes=64)
+        def quantise_x(u):
+            r = round_of(u)
+            if starts_round(u):
+                x_codes[r] = quant.tile([P, D], U32, name="x_codes", align_bytes=64, bufs=4)
+                x_scales[r] = quant.tile([P, D], U8, name="x_scales", align_bytes=64, bufs=4)
+            f_cols = block_cols(u)
             nc.vector.quantize_mx(
-                out=x_codes[r][:].bitcast(E4M3_X4),
-                scales=x_scales[r][:],
-                in_=x_grouped[r][:].rearrange("p w j -> p (w j)"),
+                out=x_codes[r][:, f_cols].bitcast(E4M3_X4),
+                scales=x_scales[r][:, f_cols],
+                in_=x_grouped[r][:, f_cols, :].rearrange("p w j -> p (w j)"),
             )
 
         def y_to_features(u):
@@ -198,13 +201,16 @@ def tile_better_transformer_t_v_kernel(
                 op0=ALU.add, op1=ALU.mult,
             )
 
-        def quantise_dy(r):
-            dy_codes[r] = quant.tile([P, D], U32, name="dy_codes", align_bytes=64)
-            dy_scales[r] = quant.tile([P, D], U8, name="dy_scales", align_bytes=64)
+        def quantise_dy(u):
+            r = round_of(u)
+            if starts_round(u):
+                dy_codes[r] = quant.tile([P, D], U32, name="dy_codes", align_bytes=64)
+                dy_scales[r] = quant.tile([P, D], U8, name="dy_scales", align_bytes=64)
+            f_cols = block_cols(u)
             nc.vector.quantize_mx(
-                out=dy_codes[r][:].bitcast(E5M2_X4),
-                scales=dy_scales[r][:],
-                in_=dy_grouped[r][:].rearrange("p w j -> p (w j)"),
+                out=dy_codes[r][:, f_cols].bitcast(E5M2_X4),
+                scales=dy_scales[r][:, f_cols],
+                in_=dy_grouped[r][:, f_cols, :].rearrange("p w j -> p (w j)"),
             )
 
         def multiply(r, first_block):
@@ -296,6 +302,8 @@ def tile_better_transformer_t_v_kernel(
 
         for u in range(X_LEAD):
             x_norm_block(u)
+        for u in range(X_LEAD - 1):
+            quantise_x(u)
         for u in range(Y_LEAD):
             y_to_features(u)
 
@@ -323,12 +331,10 @@ def tile_better_transformer_t_v_kernel(
                 finish_dy(s - FINISH_LAG)
             if is_unit(s + X_LEAD) and x_on_vector(s + X_LEAD):
                 x_norm_block(s + X_LEAD)
-            x_round = round_ending_at(s + X_LEAD - 1)
-            if x_round is not None:
-                quantise_x(x_round)
-            full_round = round_ending_at(s - MULTIPLY_LAG)
-            if full_round is not None:
-                quantise_dy(full_round)
+            if is_unit(s + X_LEAD - 1):
+                quantise_x(s + X_LEAD - 1)
+            if is_unit(s - MULTIPLY_LAG):
+                quantise_dy(s - MULTIPLY_LAG)
 
             stored_round = round_ending_at(s - STORE_LAG)
             if stored_round is not None and (stored_round + 1) % PASSES == 0:

@@ -26,14 +26,15 @@ UNITS = ROUNDS * BLOCKS
 
 Y_LEAD = 2
 X_LEAD = BLOCKS
-DAMP_SCALAR_COLS = 256
-X_SCALAR_EVERY = 3
+DAMP_SCALAR_COLS = 192
+X_SCALAR_OF_FIVE = (1, 3)
 CORRECT_LAG = 1
 BACK_LAG = 2
 FINISH_LAG = 3
 MULTIPLY_LAG = 4
 PASSES_A_STEP = 1
-STORE_LAG = 8
+COPY_LAG = 3
+STORE_LAG = 10
 LOAD_LEAD = 2
 
 FLOPS = 2 * PARTS * TOKENS * D * D
@@ -69,7 +70,7 @@ def tile_better_transformer_t_v_kernel(
             return True
 
         def x_on_vector(u):
-            return u % X_SCALAR_EVERY != X_SCALAR_EVERY - 1
+            return u % 5 not in X_SCALAR_OF_FIVE
 
         def round_of(u):
             return u // BLOCKS
@@ -229,14 +230,13 @@ def tile_better_transformer_t_v_kernel(
                     stop=(c == PASSES - 1),
                 )
 
-        def store_part(part):
-            for i in range(BLOCKS):
-                result = results.tile([P, D], F32, name="result")
-                if i % 2 == 0 and part == PARTS - 1:
-                    nc.vector.tensor_copy(out=result[:], in_=acc[part][i][:])
-                else:
-                    nc.scalar.copy(out=result[:], in_=acc[part][i][:])
-                nc.sync.dma_start(out=out[part, i * P : (i + 1) * P, :], in_=result[:])
+        def store_block(part, i):
+            result = results.tile([P, D], F32, name="result")
+            if i % 2 == 0 and part == PARTS - 1:
+                nc.vector.tensor_copy(out=result[:], in_=acc[part][i][:])
+            else:
+                nc.scalar.copy(out=result[:], in_=acc[part][i][:])
+            nc.sync.dma_start(out=out[part, i * P : (i + 1) * P, :], in_=result[:])
 
         table_in = consts.tile([P, 1], F32)
         nc.vector.memset(table_in[:], 0.0)
@@ -336,9 +336,10 @@ def tile_better_transformer_t_v_kernel(
             if is_unit(s - MULTIPLY_LAG):
                 quantise_dy(s - MULTIPLY_LAG)
 
-            stored_round = round_ending_at(s - STORE_LAG)
-            if stored_round is not None and (stored_round + 1) % PASSES == 0:
-                store_part(stored_round // PASSES)
+            for i in range(BLOCKS):
+                stored_round = round_ending_at(s - MULTIPLY_LAG - i - COPY_LAG)
+                if stored_round is not None and (stored_round + 1) % PASSES == 0:
+                    store_block(stored_round // PASSES, i)
 
             if is_unit(s - BACK_LAG):
                 corr_to_tokens(s - BACK_LAG)

@@ -26,8 +26,7 @@ UNITS = ROUNDS * BLOCKS
 
 Y_LEAD = 2
 X_LEAD = BLOCKS
-DAMP_SCALAR_COLS = 192
-X_SCALAR_OF_FIVE = (1, 3)
+DAMP_SCALAR_COLS = 128
 CORRECT_LAG = 1
 BACK_LAG = 2
 FINISH_LAG = 3
@@ -70,7 +69,7 @@ def tile_better_transformer_t_v_kernel(
             return True
 
         def x_on_vector(u):
-            return u % 5 not in X_SCALAR_OF_FIVE
+            return u % 2 == 0
 
         def round_of(u):
             return u // BLOCKS

@@ -24,16 +24,17 @@ VEC_ROWS = PARTS * BLOCKS
 ROUNDS = PARTS * PASSES
 UNITS = ROUNDS * BLOCKS
 
-Y_LEAD = 2
-X_LEAD = BLOCKS
-DAMP_SCALAR_COLS = 128
-CORRECT_LAG = 1
-BACK_LAG = 2
-FINISH_LAG = 3
-MULTIPLY_LAG = 4
-PASSES_A_STEP = 1
-COPY_LAG = 3
-STORE_LAG = 10
+SPAN = 2
+SPANS = ROUNDS // SPAN * BLOCKS
+NARROW = (0, SPANS - 2, SPANS - 1)
+X_CHUNK = SPAN * D // BLOCKS
+X_CHUNKS = D // X_CHUNK
+X_LEAD = 1
+X_VECTOR = 72
+X_WHOLE = (0, 1, 2, 21, 22)
+FINISH_LAG = 2
+PASSES_A_STEP = 2
+COPY_LAG = 2
 LOAD_LEAD = 2
 
 FLOPS = 2 * PARTS * TOKENS * D * D
@@ -49,10 +50,10 @@ def tile_better_transformer_t_v_kernel(
 
     with ExitStack() as ctx:
         consts = ctx.enter_context(tc.tile_pool(name="consts", bufs=1))
-        loads = ctx.enter_context(tc.tile_pool(name="loads", bufs=3))
+        loads = ctx.enter_context(tc.tile_pool(name="loads", bufs=6))
         work = ctx.enter_context(tc.tile_pool(name="work", bufs=3))
-        grouped = ctx.enter_context(tc.tile_pool(name="grouped", bufs=3))
-        quant = ctx.enter_context(tc.tile_pool(name="quant", bufs=3))
+        grouped = ctx.enter_context(tc.tile_pool(name="grouped", bufs=4))
+        quant = ctx.enter_context(tc.tile_pool(name="quant", bufs=6))
         results = ctx.enter_context(tc.tile_pool(name="results", bufs=BLOCKS))
         acc_pool = ctx.enter_context(tc.psum_pool(name="acc", bufs=1))
         to_features = ctx.enter_context(tc.psum_pool(name="to_features", bufs=2))
@@ -65,32 +66,35 @@ def tile_better_transformer_t_v_kernel(
         y_t, tanh_half, silu, damped, corr, corr_t = {}, {}, {}, {}, {}, {}
         acc = {}
 
-        def damp_on_scalar(u):
-            return True
+        steps = []
+        for s in range(SPANS):
+            halves = [(s, h) for h in range(SPAN)]
+            steps.extend([[u] for u in halves] if s in NARROW else [halves])
 
-        def x_on_vector(u):
-            return u % 2 == 0
+        def units(k):
+            return steps[k] if 0 <= k < len(steps) else []
 
-        def round_of(u):
-            return u // BLOCKS
+        def round_of(s, h):
+            return s // BLOCKS * SPAN + h
 
-        def starts_round(u):
-            return u % BLOCKS == 0
-
-        def block_cols(u):
-            b = u % BLOCKS
+        def cols_of(s):
+            b = s % BLOCKS
             return slice(b * P, (b + 1) * P)
 
-        def const_col(u):
-            col = u // (PASSES * BLOCKS) * BLOCKS + u % BLOCKS
+        def const_col(s):
+            col = round_of(s, 0) // PASSES * BLOCKS + s % BLOCKS
             return slice(col, col + 1)
 
-        def load_x(r):
+        def load_x(r, lo=0, width=D):
             part, c = divmod(r, PASSES)
-            x_raw[r] = loads.tile([P, PACK, D], BF16, name="x_raw", bufs=4)
-            nc.sync.dma_start(out=x_raw[r][:], in_=x_view[c, :, :, part * D : (part + 1) * D])
+            if lo == 0:
+                x_raw[r] = loads.tile([P, PACK, D], BF16, name="x_raw")
+            nc.sync.dma_start(
+                out=x_raw[r][:, :, lo : lo + width],
+                in_=x_view[c, :, :, part * D + lo : part * D + lo + width],
+            )
 
-        def load_y(r, lo, width):
+        def load_y(r, lo=0, width=D):
             part, c = divmod(r, PASSES)
             if lo == 0:
                 y_raw[r] = loads.tile([P, PACK, D], F32, name="y_raw")
@@ -101,140 +105,130 @@ def tile_better_transformer_t_v_kernel(
 
         def load_g(r):
             part, c = divmod(r, PASSES)
-            g_raw[r] = loads.tile([P, PACK, D], BF16, name="g_raw", bufs=4)
+            g_raw[r] = loads.tile([P, PACK, D], BF16, name="g_raw", bufs=8)
             nc.sync.dma_start(out=g_raw[r][:], in_=g_view[c, :, :, part * D : (part + 1) * D])
 
-        def x_norm_block(u):
-            r = round_of(u)
-            if starts_round(u):
-                x_grouped[r] = grouped.tile([P, D, PACK], BF16, name="x_grouped", align_bytes=64)
-            f_cols = block_cols(u)
-            if x_on_vector(u):
-                nc.vector.tensor_scalar(
-                    out=x_grouped[r][:, f_cols, :].rearrange("p (n i) j -> p n j i", i=4),
-                    in0=x_raw[r][:, :, f_cols].rearrange("p j (n i) -> p n j i", i=4),
-                    scalar1=gain_col[:, 0:1], scalar2=shift_col[:, 0:1],
-                    op0=ALU.mult, op1=ALU.add,
-                )
-                return
-            nc.scalar.activation(
-                out=x_grouped[r][:, f_cols, :].rearrange("p (n i) j -> p n j i", i=4),
-                in_=x_raw[r][:, :, f_cols].rearrange("p j (n i) -> p n j i", i=4),
-                func=FUNC.Identity,
-                bias=shift_col[:, 0:1],
-                scale=gain_col[:, 0:1],
+        def x_norm(q):
+            r, k = divmod(q, X_CHUNKS)
+            vector_cols = X_CHUNK if q in X_WHOLE else X_VECTOR
+            x_grouped[q] = grouped.tile([P, X_CHUNK, PACK], BF16, name="x_grouped", align_bytes=64)
+            src = x_raw[r][:, :, k * X_CHUNK : (k + 1) * X_CHUNK]
+            nc.vector.tensor_scalar(
+                out=x_grouped[q][:, 0:vector_cols, :].rearrange("p (n i) j -> p n j i", i=4),
+                in0=src[:, :, 0:vector_cols].rearrange("p j (n i) -> p n j i", i=4),
+                scalar1=gain_col[:, 0:1], scalar2=shift_col[:, 0:1],
+                op0=ALU.mult, op1=ALU.add,
             )
+            if vector_cols < X_CHUNK:
+                nc.scalar.activation(
+                    out=x_grouped[q][:, vector_cols:, :].rearrange("p (n i) j -> p n j i", i=4),
+                    in_=src[:, :, vector_cols:].rearrange("p j (n i) -> p n j i", i=4),
+                    func=FUNC.Identity,
+                    bias=shift_col[:, 0:1],
+                    scale=gain_col[:, 0:1],
+                )
 
-        def quantise_x(u):
-            r = round_of(u)
-            if starts_round(u):
-                x_codes[r] = quant.tile([P, D], U32, name="x_codes", align_bytes=64, bufs=4)
-                x_scales[r] = quant.tile([P, D], U8, name="x_scales", align_bytes=64, bufs=4)
-            f_cols = block_cols(u)
+        def quantise_x(q):
+            r, k = divmod(q, X_CHUNKS)
+            if k == 0:
+                x_codes[r] = quant.tile([P, D], U32, name="x_codes", align_bytes=64)
+                x_scales[r] = quant.tile([P, D], U8, name="x_scales", align_bytes=64)
+            f_cols = slice(k * X_CHUNK, (k + 1) * X_CHUNK)
             nc.vector.quantize_mx(
                 out=x_codes[r][:, f_cols].bitcast(E4M3_X4),
                 scales=x_scales[r][:, f_cols],
-                in_=x_grouped[r][:, f_cols, :].rearrange("p w j -> p (w j)"),
+                in_=x_grouped[q][:].rearrange("p w j -> p (w j)"),
             )
 
-        def y_to_features(u):
-            y_t[u] = to_features.tile([P, PACK, P], F32, name="y_t")
+        def y_to_features(s, h):
+            y_t[s, h] = to_features.tile([P, PACK, P], F32, name="y_t")
             for j in range(PACK):
-                nc.tensor.transpose(y_t[u][:, j, :], y_raw[round_of(u)][:, j, block_cols(u)], ident[:])
+                nc.tensor.transpose(
+                    y_t[s, h][:, j, :], y_raw[round_of(s, h)][:, j, cols_of(s)], ident[:]
+                )
 
-        def activations(u):
-            tanh_half[u] = work.tile([P, PACK, P], F32, name="tanh_half")
-            nc.scalar.activation(
-                out=tanh_half[u][:], in_=y_t[u][:], func=FUNC.Tanh,
-                scale=half_beta_col[:, const_col(u)],
-            )
-            silu[u] = work.tile([P, PACK, P], F32, name="silu")
-            nc.scalar.activation(
-                out=silu[u][:], in_=y_t[u][:], func=FUNC.Silu,
-                scale=beta_col[:, const_col(u)],
-            )
+        def step_tile(k, name, bufs):
+            return work.tile([P, len(steps[k]), PACK, P], F32, name=name, bufs=bufs)
 
-        def damp(u):
-            damped[u] = work.tile([P, PACK, P], F32, name="damped")
-            if damp_on_scalar(u):
-                damped_flat = damped[u][:].rearrange("p j f -> p (j f)")
-                tanh_flat = tanh_half[u][:].rearrange("p j f -> p (j f)")
-                nc.gpsimd.tensor_scalar(
-                    out=damped_flat[:, DAMP_SCALAR_COLS:], in0=tanh_flat[:, DAMP_SCALAR_COLS:],
-                    scalar1=damp_col[:, const_col(u)], scalar2=neg_damp_col[:, const_col(u)],
-                    op0=ALU.mult, op1=ALU.add,
+        def activations(k):
+            tanh_half[k] = step_tile(k, "tanh_half", 3)
+            silu[k] = step_tile(k, "silu", 3)
+            for n, (s, h) in enumerate(steps[k]):
+                nc.scalar.activation(
+                    out=tanh_half[k][:, n], in_=y_t[s, h][:], func=FUNC.Tanh,
+                    scale=half_beta_col[:, const_col(s)],
                 )
                 nc.scalar.activation(
-                    out=damped_flat[:, 0:DAMP_SCALAR_COLS], in_=tanh_flat[:, 0:DAMP_SCALAR_COLS],
-                    func=FUNC.Identity,
-                    scale=damp_col[:, const_col(u)], bias=neg_damp_col[:, const_col(u)],
+                    out=silu[k][:, n], in_=y_t[s, h][:], func=FUNC.Silu,
+                    scale=beta_col[:, const_col(s)],
                 )
-                return
-            nc.vector.tensor_scalar(
-                out=damped[u][:], in0=tanh_half[u][:],
-                scalar1=1.0, scalar2=damp_col[:, const_col(u)],
-                op0=ALU.subtract, op1=ALU.mult,
+
+        def damp(k):
+            s = steps[k][0][0]
+            damped[k] = step_tile(k, "damped", 2)
+            nc.gpsimd.tensor_scalar(
+                out=damped[k][:], in0=tanh_half[k][:],
+                scalar1=damp_col[:, const_col(s)], scalar2=neg_damp_col[:, const_col(s)],
+                op0=ALU.mult, op1=ALU.add,
             )
 
-        def correct(u):
-            corr[u] = work.tile([P, PACK, P], F32, name="corr")
+        def correct(k):
+            corr[k] = step_tile(k, "corr", 3)
             nc.vector.scalar_tensor_tensor(
-                out=corr[u][:], in0=silu[u][:], scalar=1.0, in1=damped[u][:],
+                out=corr[k][:], in0=silu[k][:], scalar=1.0, in1=damped[k][:],
                 op0=ALU.subtract, op1=ALU.mult,
             )
 
-        def corr_to_tokens(u):
-            corr_t[u] = to_tokens.tile([P, PACK, P], F32, name="corr_t")
+        def corr_to_tokens(k, n):
+            s, h = steps[k][n]
+            corr_t[s, h] = to_tokens.tile([P, PACK, P], F32, name="corr_t")
             for j in range(PACK):
-                nc.tensor.transpose(corr_t[u][:, j, :], corr[u][:, j, :], ident[:])
+                nc.tensor.transpose(corr_t[s, h][:, j, :], corr[k][:, n, j, :], ident[:])
 
-        def finish_dy(u):
-            r = round_of(u)
-            if starts_round(u):
+        def finish_dy(s, h):
+            r = round_of(s, h)
+            if s % BLOCKS == 0:
                 dy_grouped[r] = grouped.tile([P, D, PACK], BF16, name="dy_grouped", align_bytes=64)
-            f_cols = block_cols(u)
             nc.vector.scalar_tensor_tensor(
-                out=dy_grouped[r][:, f_cols, :],
-                in0=corr_t[u][:].rearrange("p j f -> p f j"),
+                out=dy_grouped[r][:, cols_of(s), :],
+                in0=corr_t[s, h][:].rearrange("p j f -> p f j"),
                 scalar=1.0,
-                in1=g_raw[r][:, :, f_cols].rearrange("p j f -> p f j"),
+                in1=g_raw[r][:, :, cols_of(s)].rearrange("p j f -> p f j"),
                 op0=ALU.add, op1=ALU.mult,
             )
 
-        def quantise_dy(u):
-            r = round_of(u)
-            if starts_round(u):
+        def quantise_dy(r, first, count):
+            if first == 0:
                 dy_codes[r] = quant.tile([P, D], U32, name="dy_codes", align_bytes=64)
                 dy_scales[r] = quant.tile([P, D], U8, name="dy_scales", align_bytes=64)
-            f_cols = block_cols(u)
+            f_cols = slice(first * P, (first + count) * P)
             nc.vector.quantize_mx(
                 out=dy_codes[r][:, f_cols].bitcast(E5M2_X4),
                 scales=dy_scales[r][:, f_cols],
                 in_=dy_grouped[r][:, f_cols, :].rearrange("p w j -> p (w j)"),
             )
 
-        def multiply(r, first_block):
+        def multiply(r, i):
             part, c = divmod(r, PASSES)
-            if c == 0 and first_block == 0:
-                acc[part] = [acc_pool.tile([P, D], F32, name="acc%d" % i) for i in range(BLOCKS)]
-            for i in range(first_block, first_block + PASSES_A_STEP):
-                i_cols = slice(i * P, (i + 1) * P)
-                nc.tensor.matmul_mx(
-                    out=acc[part][i][:],
-                    lhsT=x_codes[r][:, i_cols].bitcast(E4M3_X4),
-                    lhsT_scale=x_scales[r][:, i_cols],
-                    rhs=dy_codes[r][:].bitcast(E5M2_X4),
-                    rhs_scale=dy_scales[r][:],
-                    start=(c == 0),
-                    stop=(c == PASSES - 1),
-                )
+            if c == 0:
+                acc[part, i] = acc_pool.tile([P, D], F32, name="acc%d" % i)
+            i_cols = slice(i * P, (i + 1) * P)
+            nc.tensor.matmul_mx(
+                out=acc[part, i][:],
+                lhsT=x_codes[r][:, i_cols].bitcast(E4M3_X4),
+                lhsT_scale=x_scales[r][:, i_cols],
+                rhs=dy_codes[r][:].bitcast(E5M2_X4),
+                rhs_scale=dy_scales[r][:],
+                start=(c == 0),
+                stop=(c == PASSES - 1),
+            )
 
         def store_block(part, i):
             result = results.tile([P, D], F32, name="result")
             if i % 2 == 0 and part == PARTS - 1:
-                nc.vector.tensor_copy(out=result[:], in_=acc[part][i][:])
+                nc.vector.tensor_copy(out=result[:], in_=acc[part, i][:])
             else:
-                nc.scalar.copy(out=result[:], in_=acc[part][i][:])
+                nc.scalar.copy(out=result[:], in_=acc[part, i][:])
             nc.sync.dma_start(out=out[part, i * P : (i + 1) * P, :], in_=result[:])
 
         table_in = consts.tile([P, 1], F32)
@@ -255,18 +249,26 @@ def tile_better_transformer_t_v_kernel(
             out=vec_bf[VEC_ROWS : 2 * VEC_ROWS, :], in_=gamma.rearrange("(r f) -> r f", f=P)
         )
         load_y(0, 0, P)
-        load_x(0)
+        load_x(0, 0, X_CHUNK)
+        load_y(1, 0, P)
+        load_x(0, X_CHUNK, X_CHUNK)
         load_y(0, P, P)
+        load_y(1, P, P)
         load_x(1)
         load_y(0, 2 * P, P)
-        load_y(0, 3 * P, P)
-        load_g(0)
-        load_y(1, 0, P)
-        load_y(1, P, P)
-        load_x(2)
         load_y(1, 2 * P, P)
-        load_y(1, 3 * P, P)
+        load_g(0)
         load_g(1)
+        load_y(0, 3 * P, P)
+        load_y(1, 3 * P, P)
+        load_x(2)
+        load_y(2, 0, 2 * P)
+        load_y(3, 0, 2 * P)
+        load_y(2, 2 * P, 2 * P)
+        load_y(3, 2 * P, 2 * P)
+        load_x(3)
+        load_g(2)
+        load_g(3)
 
         gain_col = consts.tile([P, 1], F32)
         nc.vector.tensor_copy(out=gain_col[:], in_=gain_bf[:])
@@ -293,58 +295,63 @@ def tile_better_transformer_t_v_kernel(
             scalar1=-0.5, scalar2=0.5, op0=ALU.mult, op1=ALU.add,
         )
 
-        def is_unit(u):
-            return 0 <= u < UNITS
+        x_norm(0)
+        for s, h in units(0):
+            y_to_features(s, h)
 
-        def round_ending_at(u):
-            return round_of(u) if is_unit(u) and starts_round(u + 1) else None
+        to_quantise = []
+        to_multiply = []
+        to_store = []
+        for k in range(len(steps) + FINISH_LAG):
+            ready = len(to_multiply)
+            first_s = [s for s, h in units(k) if h == 0]
+            for s in first_s:
+                pair = s // BLOCKS + LOAD_LEAD
+                if s % BLOCKS == 0 and pair < ROUNDS // SPAN:
+                    for load in (load_y, load_x, load_g):
+                        for h in range(SPAN):
+                            load(pair * SPAN + h)
 
-        for u in range(X_LEAD):
-            x_norm_block(u)
-        for u in range(X_LEAD - 1):
-            quantise_x(u)
-        for u in range(Y_LEAD):
-            y_to_features(u)
+            while to_store and to_store[0][0] <= k:
+                step, part, i = to_store.pop(0)
+                store_block(part, i)
+            if units(k):
+                activations(k)
 
-        for s in range(UNITS + STORE_LAG + 1):
-            if starts_round(s):
-                if round_of(s) + LOAD_LEAD < ROUNDS:
-                    load_y(round_of(s) + LOAD_LEAD, 0, D)
-                if round_of(s) + LOAD_LEAD + 1 < ROUNDS:
-                    load_x(round_of(s) + LOAD_LEAD + 1)
-                if round_of(s) + LOAD_LEAD < ROUNDS:
-                    load_g(round_of(s) + LOAD_LEAD)
-
-            if is_unit(s):
-                activations(s)
-                if damp_on_scalar(s):
-                    damp(s)
-            if is_unit(s + X_LEAD) and not x_on_vector(s + X_LEAD):
-                x_norm_block(s + X_LEAD)
-
-            if is_unit(s) and not damp_on_scalar(s):
-                damp(s)
-            if is_unit(s - CORRECT_LAG):
-                correct(s - CORRECT_LAG)
-            if is_unit(s - FINISH_LAG):
-                finish_dy(s - FINISH_LAG)
-            if is_unit(s + X_LEAD) and x_on_vector(s + X_LEAD):
-                x_norm_block(s + X_LEAD)
-            if is_unit(s + X_LEAD - 1):
+            if units(k - 1):
+                correct(k - 1)
+            if units(k):
+                damp(k)
+            done = units(k - FINISH_LAG)
+            for n, (s, h) in enumerate(done):
+                finish_dy(s, h)
+                r, b = round_of(s, h), s % BLOCKS
+                job = []
+                if s >= SPANS - 2:
+                    job = [(r, b, 1)]
+                elif b % 2 == 1:
+                    job = [(r, b - 1, 2)]
+                if n == 0:
+                    to_quantise.extend(job)
+            for s in first_s:
+                if s + X_LEAD < SPANS:
+                    x_norm(s + X_LEAD)
                 quantise_x(s + X_LEAD - 1)
-            if is_unit(s - MULTIPLY_LAG):
-                quantise_dy(s - MULTIPLY_LAG)
+            for r, first, count in to_quantise:
+                quantise_dy(r, first, count)
+                if first + count == BLOCKS:
+                    to_multiply.extend([(r, i) for i in range(BLOCKS)])
+            to_quantise = job if len(done) == SPAN else []
 
-            for i in range(BLOCKS):
-                stored_round = round_ending_at(s - MULTIPLY_LAG - i - COPY_LAG)
-                if stored_round is not None and (stored_round + 1) % PASSES == 0:
-                    store_block(stored_round // PASSES, i)
-
-            if is_unit(s - BACK_LAG):
-                corr_to_tokens(s - BACK_LAG)
-            if is_unit(s + Y_LEAD):
-                y_to_features(s + Y_LEAD)
-            for first_block in range(0, BLOCKS, PASSES_A_STEP):
-                ready_round = round_ending_at(s - MULTIPLY_LAG - first_block // PASSES_A_STEP)
-                if ready_round is not None:
-                    multiply(ready_round, first_block)
+            for n in range(SPAN):
+                if n < len(units(k + 1)):
+                    y_to_features(*units(k + 1)[n])
+                if n < len(units(k - 1)):
+                    corr_to_tokens(k - 1, n)
+            for n in range(min(len(to_multiply), PASSES_A_STEP, ready) if units(k) else len(to_multiply)):
+                r, i = to_multiply.pop(0)
+                multiply(r, i)
+                if r == ROUNDS - 1:
+                    store_block(PARTS - 1, i)
+                elif (r + 1) % PASSES == 0:
+                    to_store.append((k + COPY_LAG, r // PASSES, i))

@@ -25,17 +25,18 @@ ROUNDS = PARTS * PASSES
 UNITS = ROUNDS * BLOCKS
 
 SPAN = 2
-SPANS = ROUNDS // SPAN * BLOCKS
-NARROW = (0, SPANS - 2, SPANS - 1)
+SPANS = ROUNDS * BLOCKS // SPAN
+NARROW = (SPANS - 1,)
 X_CHUNK = SPAN * D // BLOCKS
 X_CHUNKS = D // X_CHUNK
-X_LEAD = 1
-X_VECTOR = 72
-X_WHOLE = (0, 1, 2, 21, 22)
+GPSIMD_DAMP = 416
+X_LEAD = 0
+X_VECTOR = 112
+X_WHOLE = ()
 FINISH_LAG = 2
 PASSES_A_STEP = 2
 COPY_LAG = 2
-LOAD_LEAD = 2
+LOAD_LEAD = 3
 
 FLOPS = 2 * PARTS * TOKENS * D * D
 
@@ -74,15 +75,18 @@ def tile_better_transformer_t_v_kernel(
         def units(k):
             return steps[k] if 0 <= k < len(steps) else []
 
-        def round_of(s, h):
-            return s // BLOCKS * SPAN + h
+        def round_of(s):
+            return s * SPAN // BLOCKS
 
-        def cols_of(s):
-            b = s % BLOCKS
+        def block_of(s, h):
+            return s * SPAN % BLOCKS + h
+
+        def cols_of(s, h):
+            b = block_of(s, h)
             return slice(b * P, (b + 1) * P)
 
-        def const_col(s):
-            col = round_of(s, 0) // PASSES * BLOCKS + s % BLOCKS
+        def const_col(s, h):
+            col = round_of(s) // PASSES * BLOCKS + block_of(s, h)
             return slice(col, col + 1)
 
         def load_x(r, lo=0, width=D):
@@ -144,7 +148,7 @@ def tile_better_transformer_t_v_kernel(
             y_t[s, h] = to_features.tile([P, PACK, P], F32, name="y_t")
             for j in range(PACK):
                 nc.tensor.transpose(
-                    y_t[s, h][:, j, :], y_raw[round_of(s, h)][:, j, cols_of(s)], ident[:]
+                    y_t[s, h][:, j, :], y_raw[round_of(s)][:, j, cols_of(s, h)], ident[:]
                 )
 
         def step_tile(k, name, bufs):
@@ -156,21 +160,29 @@ def tile_better_transformer_t_v_kernel(
             for n, (s, h) in enumerate(steps[k]):
                 nc.scalar.activation(
                     out=tanh_half[k][:, n], in_=y_t[s, h][:], func=FUNC.Tanh,
-                    scale=half_beta_col[:, const_col(s)],
+                    scale=half_beta_col[:, const_col(s, h)],
                 )
                 nc.scalar.activation(
                     out=silu[k][:, n], in_=y_t[s, h][:], func=FUNC.Silu,
-                    scale=beta_col[:, const_col(s)],
+                    scale=beta_col[:, const_col(s, h)],
                 )
 
         def damp(k):
-            s = steps[k][0][0]
             damped[k] = step_tile(k, "damped", 2)
-            nc.gpsimd.tensor_scalar(
-                out=damped[k][:], in0=tanh_half[k][:],
-                scalar1=damp_col[:, const_col(s)], scalar2=neg_damp_col[:, const_col(s)],
-                op0=ALU.mult, op1=ALU.add,
-            )
+            for n, (s, h) in enumerate(steps[k]):
+                cols = (slice(0, GPSIMD_DAMP), slice(GPSIMD_DAMP, PACK * P))
+                out_flat = damped[k][:, n].rearrange("p j f -> p (j f)")
+                in_flat = tanh_half[k][:, n].rearrange("p j f -> p (j f)")
+                nc.gpsimd.tensor_scalar(
+                    out=out_flat[:, cols[0]], in0=in_flat[:, cols[0]],
+                    scalar1=damp_col[:, const_col(s, h)], scalar2=neg_damp_col[:, const_col(s, h)],
+                    op0=ALU.mult, op1=ALU.add,
+                )
+                if GPSIMD_DAMP < PACK * P:
+                    nc.scalar.activation(
+                        out=out_flat[:, cols[1]], in_=in_flat[:, cols[1]], func=FUNC.Identity,
+                        scale=damp_col[:, const_col(s, h)], bias=neg_damp_col[:, const_col(s, h)],
+                    )
 
         def correct(k):
             corr[k] = step_tile(k, "corr", 3)
@@ -186,14 +198,14 @@ def tile_better_transformer_t_v_kernel(
                 nc.tensor.transpose(corr_t[s, h][:, j, :], corr[k][:, n, j, :], ident[:])
 
         def finish_dy(s, h):
-            r = round_of(s, h)
-            if s % BLOCKS == 0:
+            r = round_of(s)
+            if block_of(s, h) == 0:
                 dy_grouped[r] = grouped.tile([P, D, PACK], BF16, name="dy_grouped", align_bytes=64)
             nc.vector.scalar_tensor_tensor(
-                out=dy_grouped[r][:, cols_of(s), :],
+                out=dy_grouped[r][:, cols_of(s, h), :],
                 in0=corr_t[s, h][:].rearrange("p j f -> p f j"),
                 scalar=1.0,
-                in1=g_raw[r][:, :, cols_of(s)].rearrange("p j f -> p f j"),
+                in1=g_raw[r][:, :, cols_of(s, h)].rearrange("p j f -> p f j"),
                 op0=ALU.add, op1=ALU.mult,
             )
 
@@ -249,27 +261,17 @@ def tile_better_transformer_t_v_kernel(
             out=vec_bf[VEC_ROWS : 2 * VEC_ROWS, :], in_=gamma.rearrange("(r f) -> r f", f=P)
         )
         load_y(0, 0, P)
-        load_x(0, 0, X_CHUNK)
-        load_y(1, 0, P)
-        load_x(0, X_CHUNK, X_CHUNK)
         load_y(0, P, P)
-        load_y(1, P, P)
-        load_x(1)
-        load_y(0, 2 * P, P)
-        load_y(1, 2 * P, P)
+        load_x(0)
+        load_y(0, 2 * P, 2 * P)
         load_g(0)
+        load_y(1, 0, 2 * P)
+        load_x(1)
+        load_y(1, 2 * P, 2 * P)
         load_g(1)
-        load_y(0, 3 * P, P)
-        load_y(1, 3 * P, P)
+        load_y(2)
         load_x(2)
-        load_y(2, 0, 2 * P)
-        load_y(3, 0, 2 * P)
-        load_y(2, 2 * P, 2 * P)
-        load_y(3, 2 * P, 2 * P)
-        load_x(3)
         load_g(2)
-        load_g(3)
-
         gain_col = consts.tile([P, 1], F32)
         nc.vector.tensor_copy(out=gain_col[:], in_=gain_bf[:])
         shift_col = consts.tile([P, 1], F32)
@@ -295,7 +297,10 @@ def tile_better_transformer_t_v_kernel(
             scalar1=-0.5, scalar2=0.5, op0=ALU.mult, op1=ALU.add,
         )
 
-        x_norm(0)
+        for q in range(X_LEAD):
+            x_norm(q)
+        for q in range(X_LEAD - 1):
+            quantise_x(q)
         for s, h in units(0):
             y_to_features(s, h)
 
@@ -306,11 +311,11 @@ def tile_better_transformer_t_v_kernel(
             ready = len(to_multiply)
             first_s = [s for s, h in units(k) if h == 0]
             for s in first_s:
-                pair = s // BLOCKS + LOAD_LEAD
-                if s % BLOCKS == 0 and pair < ROUNDS // SPAN:
-                    for load in (load_y, load_x, load_g):
-                        for h in range(SPAN):
-                            load(pair * SPAN + h)
+                r = round_of(s) + LOAD_LEAD
+                if block_of(s, 0) == 0 and r < ROUNDS:
+                    load_y(r)
+                    load_x(r)
+                    load_g(r)
 
             while to_store and to_store[0][0] <= k:
                 step, part, i = to_store.pop(0)
@@ -325,23 +330,23 @@ def tile_better_transformer_t_v_kernel(
             done = units(k - FINISH_LAG)
             for n, (s, h) in enumerate(done):
                 finish_dy(s, h)
-                r, b = round_of(s, h), s % BLOCKS
-                job = []
-                if s >= SPANS - 2:
-                    job = [(r, b, 1)]
-                elif b % 2 == 1:
-                    job = [(r, b - 1, 2)]
-                if n == 0:
-                    to_quantise.extend(job)
-            for s in first_s:
-                if s + X_LEAD < SPANS:
-                    x_norm(s + X_LEAD)
-                quantise_x(s + X_LEAD - 1)
+                r, b = round_of(s), block_of(s, h)
+                if s == SPANS - 1:
+                    to_quantise.append((r, b, 1))
+                elif h == SPAN - 1:
+                    to_quantise.append((r, b - 1, 2))
+            q = first_s[0] + X_LEAD if first_s else (SPANS if k == len(steps) else None)
+            if k >= len(steps): q = SPANS + X_LEAD + k - len(steps)
+            if q is not None:
+                if 0 <= q < SPANS and (X_LEAD <= 0 or q >= X_LEAD):
+                    x_norm(q)
+                if 0 <= q - 1 < SPANS:
+                    quantise_x(q - 1)
             for r, first, count in to_quantise:
                 quantise_dy(r, first, count)
                 if first + count == BLOCKS:
                     to_multiply.extend([(r, i) for i in range(BLOCKS)])
-            to_quantise = job if len(done) == SPAN else []
+            to_quantise = []
 
             for n in range(SPAN):
                 if n < len(units(k + 1)):

@@ -22,21 +22,20 @@ PASSES = TOKENS // K_PASS
 BLOCKS = D // P
 VEC_ROWS = PARTS * BLOCKS
 ROUNDS = PARTS * PASSES
-UNITS = ROUNDS * BLOCKS
+BANK = PACK * P
 
-SPAN = 2
-SPANS = ROUNDS * BLOCKS // SPAN
-NARROW = (SPANS - 1,)
-X_CHUNK = SPAN * D // BLOCKS
-X_CHUNKS = D // X_CHUNK
-GPSIMD_DAMP = 416
-X_LEAD = 0
-X_VECTOR = 112
-X_WHOLE = ()
+STEP_BLOCKS = 2
+STEPS_A_ROUND = BLOCKS // STEP_BLOCKS
+X_CHUNK = STEP_BLOCKS * P
+
+CORRECT_LAG = 1
 FINISH_LAG = 2
 PASSES_A_STEP = 2
 COPY_LAG = 2
 LOAD_LEAD = 3
+DAMP_SCALAR_COLS = 192
+X_VECTOR = 96
+X_FILL = 3
 
 FLOPS = 2 * PARTS * TOKENS * D * D
 
@@ -61,127 +60,126 @@ def tile_better_transformer_t_v_kernel(
         to_tokens = ctx.enter_context(tc.psum_pool(name="to_tokens", bufs=2))
         ctx.enter_context(tc.manual_schedule())
 
-        x_raw, y_raw, g_raw = {}, {}, {}
-        x_grouped, x_codes, x_scales = {}, {}, {}
-        dy_grouped, dy_codes, dy_scales = {}, {}, {}
-        y_t, tanh_half, silu, damped, corr, corr_t = {}, {}, {}, {}, {}, {}
-        acc = {}
-
         steps = []
-        for s in range(SPANS):
-            halves = [(s, h) for h in range(SPAN)]
-            steps.extend([[u] for u in halves] if s in NARROW else [halves])
+        for r in range(ROUNDS):
+            for b in range(0, BLOCKS, STEP_BLOCKS):
+                steps.append([(r, b + n) for n in range(STEP_BLOCKS)])
+        last_units = steps.pop()
+        steps.extend([u] for u in last_units)
 
         def units(k):
             return steps[k] if 0 <= k < len(steps) else []
 
-        def round_of(s):
-            return s * SPAN // BLOCKS
+        x_raw, y_raw, g_raw = {}, {}, {}
+        x_grouped, x_codes, x_scales = {}, {}, {}
+        dy_grouped, dy_codes, dy_scales = {}, {}, {}
+        y_t, corr_t = {}, {}
+        tanh_half, silu, damped, corr = {}, {}, {}, {}
+        acc = {}
 
-        def block_of(s, h):
-            return s * SPAN % BLOCKS + h
-
-        def cols_of(s, h):
-            b = block_of(s, h)
+        def block_cols(b):
             return slice(b * P, (b + 1) * P)
 
-        def const_col(s, h):
-            col = round_of(s) // PASSES * BLOCKS + block_of(s, h)
+        def const_col(r, b):
+            col = r // PASSES * BLOCKS + b
             return slice(col, col + 1)
 
-        def load_x(r, lo=0, width=D):
+        def load(raw, view, dtype, name, bufs, r, lo, width):
             part, c = divmod(r, PASSES)
             if lo == 0:
-                x_raw[r] = loads.tile([P, PACK, D], BF16, name="x_raw")
+                raw[r] = loads.tile([P, PACK, D], dtype, name=name, bufs=bufs)
             nc.sync.dma_start(
-                out=x_raw[r][:, :, lo : lo + width],
-                in_=x_view[c, :, :, part * D + lo : part * D + lo + width],
+                out=raw[r][:, :, lo : lo + width],
+                in_=view[c, :, :, part * D + lo : part * D + lo + width],
             )
+
+        def load_x(r):
+            load(x_raw, x_view, BF16, "x_raw", 6, r, 0, D)
 
         def load_y(r, lo=0, width=D):
-            part, c = divmod(r, PASSES)
-            if lo == 0:
-                y_raw[r] = loads.tile([P, PACK, D], F32, name="y_raw")
-            nc.sync.dma_start(
-                out=y_raw[r][:, :, lo : lo + width],
-                in_=y_view[c, :, :, part * D + lo : part * D + lo + width],
-            )
+            load(y_raw, y_view, F32, "y_raw", 6, r, lo, width)
 
         def load_g(r):
-            part, c = divmod(r, PASSES)
-            g_raw[r] = loads.tile([P, PACK, D], BF16, name="g_raw", bufs=8)
-            nc.sync.dma_start(out=g_raw[r][:], in_=g_view[c, :, :, part * D : (part + 1) * D])
+            load(g_raw, g_view, BF16, "g_raw", 8, r, 0, D)
 
-        def x_norm(q):
-            r, k = divmod(q, X_CHUNKS)
-            vector_cols = X_CHUNK if q in X_WHOLE else X_VECTOR
-            x_grouped[q] = grouped.tile([P, X_CHUNK, PACK], BF16, name="x_grouped", align_bytes=64)
-            src = x_raw[r][:, :, k * X_CHUNK : (k + 1) * X_CHUNK]
+        def x_norm(q, vector_cols):
+            r, half = divmod(q, STEPS_A_ROUND)
+            if half == 0:
+                x_grouped[r] = grouped.tile([P, D, PACK], BF16, name="x_grouped", align_bytes=64)
+            lo = half * X_CHUNK
+            cut = lo + vector_cols
+            hi = lo + X_CHUNK
             nc.vector.tensor_scalar(
-                out=x_grouped[q][:, 0:vector_cols, :].rearrange("p (n i) j -> p n j i", i=4),
-                in0=src[:, :, 0:vector_cols].rearrange("p j (n i) -> p n j i", i=4),
+                out=x_grouped[r][:, lo:cut, :].rearrange("p (n i) j -> p n j i", i=4),
+                in0=x_raw[r][:, :, lo:cut].rearrange("p j (n i) -> p n j i", i=4),
                 scalar1=gain_col[:, 0:1], scalar2=shift_col[:, 0:1],
                 op0=ALU.mult, op1=ALU.add,
             )
-            if vector_cols < X_CHUNK:
+            if cut < hi:
                 nc.scalar.activation(
-                    out=x_grouped[q][:, vector_cols:, :].rearrange("p (n i) j -> p n j i", i=4),
-                    in_=src[:, :, vector_cols:].rearrange("p j (n i) -> p n j i", i=4),
+                    out=x_grouped[r][:, cut:hi, :].rearrange("p (n i) j -> p n j i", i=4),
+                    in_=x_raw[r][:, :, cut:hi].rearrange("p j (n i) -> p n j i", i=4),
                     func=FUNC.Identity,
                     bias=shift_col[:, 0:1],
                     scale=gain_col[:, 0:1],
                 )
 
-        def quantise_x(q):
-            r, k = divmod(q, X_CHUNKS)
-            if k == 0:
-                x_codes[r] = quant.tile([P, D], U32, name="x_codes", align_bytes=64)
-                x_scales[r] = quant.tile([P, D], U8, name="x_scales", align_bytes=64)
-            f_cols = slice(k * X_CHUNK, (k + 1) * X_CHUNK)
+        def quantise(src, codes, scales, dtype, name, r, first, count):
+            if first == 0:
+                codes[r] = quant.tile([P, D], U32, name=name + "_codes", align_bytes=64)
+                scales[r] = quant.tile([P, D], U8, name=name + "_scales", align_bytes=64)
+            cols = slice(first * P, (first + count) * P)
             nc.vector.quantize_mx(
-                out=x_codes[r][:, f_cols].bitcast(E4M3_X4),
-                scales=x_scales[r][:, f_cols],
-                in_=x_grouped[q][:].rearrange("p w j -> p (w j)"),
+                out=codes[r][:, cols].bitcast(dtype),
+                scales=scales[r][:, cols],
+                in_=src[r][:, cols, :].rearrange("p w j -> p (w j)"),
             )
 
-        def y_to_features(s, h):
-            y_t[s, h] = to_features.tile([P, PACK, P], F32, name="y_t")
+        def quantise_x(r):
+            quantise(x_grouped, x_codes, x_scales, E4M3_X4, "x", r, 0, BLOCKS)
+
+        def quantise_dy(r, first, count):
+            quantise(dy_grouped, dy_codes, dy_scales, E5M2_X4, "dy", r, first, count)
+
+        def y_to_features(r, b):
+            y_t[r, b] = to_features.tile([P, PACK, P], F32, name="y_t")
             for j in range(PACK):
-                nc.tensor.transpose(
-                    y_t[s, h][:, j, :], y_raw[round_of(s)][:, j, cols_of(s, h)], ident[:]
-                )
+                nc.tensor.transpose(y_t[r, b][:, j, :], y_raw[r][:, j, block_cols(b)], ident[:])
 
         def step_tile(k, name, bufs):
-            return work.tile([P, len(steps[k]), PACK, P], F32, name=name, bufs=bufs)
+            return work.tile([P, len(steps[k]) * BANK], F32, name=name, bufs=bufs)
+
+        def unit_cols(n):
+            return slice(n * BANK, (n + 1) * BANK)
 
         def activations(k):
-            tanh_half[k] = step_tile(k, "tanh_half", 3)
-            silu[k] = step_tile(k, "silu", 3)
-            for n, (s, h) in enumerate(steps[k]):
-                nc.scalar.activation(
-                    out=tanh_half[k][:, n], in_=y_t[s, h][:], func=FUNC.Tanh,
-                    scale=half_beta_col[:, const_col(s, h)],
-                )
-                nc.scalar.activation(
-                    out=silu[k][:, n], in_=y_t[s, h][:], func=FUNC.Silu,
-                    scale=beta_col[:, const_col(s, h)],
-                )
+            for tiles, name, func, scale_col in (
+                (tanh_half, "tanh_half", FUNC.Tanh, half_beta_col),
+                (silu, "silu", FUNC.Silu, beta_col),
+            ):
+                tiles[k] = step_tile(k, name, 3)
+                for n, (r, b) in enumerate(steps[k]):
+                    nc.scalar.activation(
+                        out=tiles[k][:, unit_cols(n)],
+                        in_=y_t[r, b][:].rearrange("p j f -> p (j f)"),
+                        func=func, scale=scale_col[:, const_col(r, b)],
+                    )
 
         def damp(k):
             damped[k] = step_tile(k, "damped", 2)
-            for n, (s, h) in enumerate(steps[k]):
-                cols = (slice(0, GPSIMD_DAMP), slice(GPSIMD_DAMP, PACK * P))
-                out_flat = damped[k][:, n].rearrange("p j f -> p (j f)")
-                in_flat = tanh_half[k][:, n].rearrange("p j f -> p (j f)")
+            scalar_cols = DAMP_SCALAR_COLS * len(steps[k]) // STEP_BLOCKS
+            for n, (r, b) in enumerate(steps[k]):
+                lo, hi = unit_cols(n).start, unit_cols(n).stop
+                cut = hi - scalar_cols if n == len(steps[k]) - 1 else hi
+                scale, shift = damp_col[:, const_col(r, b)], neg_damp_col[:, const_col(r, b)]
                 nc.gpsimd.tensor_scalar(
-                    out=out_flat[:, cols[0]], in0=in_flat[:, cols[0]],
-                    scalar1=damp_col[:, const_col(s, h)], scalar2=neg_damp_col[:, const_col(s, h)],
-                    op0=ALU.mult, op1=ALU.add,
+                    out=damped[k][:, lo:cut], in0=tanh_half[k][:, lo:cut],
+                    scalar1=scale, scalar2=shift, op0=ALU.mult, op1=ALU.add,
                 )
-                if GPSIMD_DAMP < PACK * P:
+                if cut < hi:
                     nc.scalar.activation(
-                        out=out_flat[:, cols[1]], in_=in_flat[:, cols[1]], func=FUNC.Identity,
-                        scale=damp_col[:, const_col(s, h)], bias=neg_damp_col[:, const_col(s, h)],
+                        out=damped[k][:, cut:hi], in_=tanh_half[k][:, cut:hi],
+                        func=FUNC.Identity, scale=scale, bias=shift,
                     )
 
         def correct(k):
@@ -192,43 +190,31 @@ def tile_better_transformer_t_v_kernel(
             )
 
         def corr_to_tokens(k, n):
-            s, h = steps[k][n]
-            corr_t[s, h] = to_tokens.tile([P, PACK, P], F32, name="corr_t")
+            r, b = steps[k][n]
+            corr_t[r, b] = to_tokens.tile([P, PACK, P], F32, name="corr_t")
             for j in range(PACK):
-                nc.tensor.transpose(corr_t[s, h][:, j, :], corr[k][:, n, j, :], ident[:])
+                lo = unit_cols(n).start + j * P
+                nc.tensor.transpose(corr_t[r, b][:, j, :], corr[k][:, lo : lo + P], ident[:])
 
-        def finish_dy(s, h):
-            r = round_of(s)
-            if block_of(s, h) == 0:
+        def finish_dy(r, b):
+            if b == 0:
                 dy_grouped[r] = grouped.tile([P, D, PACK], BF16, name="dy_grouped", align_bytes=64)
             nc.vector.scalar_tensor_tensor(
-                out=dy_grouped[r][:, cols_of(s, h), :],
-                in0=corr_t[s, h][:].rearrange("p j f -> p f j"),
+                out=dy_grouped[r][:, block_cols(b), :],
+                in0=corr_t[r, b][:].rearrange("p j f -> p f j"),
                 scalar=1.0,
-                in1=g_raw[r][:, :, cols_of(s, h)].rearrange("p j f -> p f j"),
+                in1=g_raw[r][:, :, block_cols(b)].rearrange("p j f -> p f j"),
                 op0=ALU.add, op1=ALU.mult,
-            )
-
-        def quantise_dy(r, first, count):
-            if first == 0:
-                dy_codes[r] = quant.tile([P, D], U32, name="dy_codes", align_bytes=64)
-                dy_scales[r] = quant.tile([P, D], U8, name="dy_scales", align_bytes=64)
-            f_cols = slice(first * P, (first + count) * P)
-            nc.vector.quantize_mx(
-                out=dy_codes[r][:, f_cols].bitcast(E5M2_X4),
-                scales=dy_scales[r][:, f_cols],
-                in_=dy_grouped[r][:, f_cols, :].rearrange("p w j -> p (w j)"),
             )
 
         def multiply(r, i):
             part, c = divmod(r, PASSES)
             if c == 0:
                 acc[part, i] = acc_pool.tile([P, D], F32, name="acc%d" % i)
-            i_cols = slice(i * P, (i + 1) * P)
             nc.tensor.matmul_mx(
                 out=acc[part, i][:],
-                lhsT=x_codes[r][:, i_cols].bitcast(E4M3_X4),
-                lhsT_scale=x_scales[r][:, i_cols],
+                lhsT=x_codes[r][:, block_cols(i)].bitcast(E4M3_X4),
+                lhsT_scale=x_scales[r][:, block_cols(i)],
                 rhs=dy_codes[r][:].bitcast(E5M2_X4),
                 rhs_scale=dy_scales[r][:],
                 start=(c == 0),
@@ -272,6 +258,7 @@ def tile_better_transformer_t_v_kernel(
         load_y(2)
         load_x(2)
         load_g(2)
+
         gain_col = consts.tile([P, 1], F32)
         nc.vector.tensor_copy(out=gain_col[:], in_=gain_bf[:])
         shift_col = consts.tile([P, 1], F32)
@@ -297,66 +284,57 @@ def tile_better_transformer_t_v_kernel(
             scalar1=-0.5, scalar2=0.5, op0=ALU.mult, op1=ALU.add,
         )
 
-        for q in range(X_LEAD):
-            x_norm(q)
-        for q in range(X_LEAD - 1):
-            quantise_x(q)
-        for s, h in units(0):
-            y_to_features(s, h)
+        for u in units(0):
+            y_to_features(*u)
 
         to_quantise = []
         to_multiply = []
         to_store = []
         for k in range(len(steps) + FINISH_LAG):
             ready = len(to_multiply)
-            first_s = [s for s, h in units(k) if h == 0]
-            for s in first_s:
-                r = round_of(s) + LOAD_LEAD
-                if block_of(s, 0) == 0 and r < ROUNDS:
-                    load_y(r)
-                    load_x(r)
-                    load_g(r)
+            starts_round = k % STEPS_A_ROUND == 0
+            if starts_round and k // STEPS_A_ROUND + LOAD_LEAD < ROUNDS:
+                load_y(k // STEPS_A_ROUND + LOAD_LEAD)
+                load_x(k // STEPS_A_ROUND + LOAD_LEAD)
+                load_g(k // STEPS_A_ROUND + LOAD_LEAD)
 
             while to_store and to_store[0][0] <= k:
-                step, part, i = to_store.pop(0)
-                store_block(part, i)
+                store_block(*to_store.pop(0)[1:])
             if units(k):
                 activations(k)
 
-            if units(k - 1):
-                correct(k - 1)
+            if units(k - CORRECT_LAG):
+                correct(k - CORRECT_LAG)
             if units(k):
                 damp(k)
-            done = units(k - FINISH_LAG)
-            for n, (s, h) in enumerate(done):
-                finish_dy(s, h)
-                r, b = round_of(s), block_of(s, h)
-                if s == SPANS - 1:
+            for r, b in units(k - FINISH_LAG):
+                finish_dy(r, b)
+                if r < ROUNDS - 1 and b == BLOCKS - 1:
+                    to_quantise.append((r, 0, BLOCKS))
+                elif r == ROUNDS - 1 and b % STEP_BLOCKS == 1 and b < BLOCKS - 1:
+                    to_quantise.append((r, b - 1, STEP_BLOCKS))
+                elif r == ROUNDS - 1 and b >= BLOCKS - STEP_BLOCKS:
                     to_quantise.append((r, b, 1))
-                elif h == SPAN - 1:
-                    to_quantise.append((r, b - 1, 2))
-            q = first_s[0] + X_LEAD if first_s else (SPANS if k == len(steps) else None)
-            if k >= len(steps): q = SPANS + X_LEAD + k - len(steps)
-            if q is not None:
-                if 0 <= q < SPANS and (X_LEAD <= 0 or q >= X_LEAD):
-                    x_norm(q)
-                if 0 <= q - 1 < SPANS:
-                    quantise_x(q - 1)
+            if k < ROUNDS * STEPS_A_ROUND:
+                x_norm(k, X_CHUNK if k < X_FILL or to_store else X_VECTOR)
+            if starts_round and 0 < k <= ROUNDS * STEPS_A_ROUND:
+                quantise_x(k // STEPS_A_ROUND - 1)
             for r, first, count in to_quantise:
                 quantise_dy(r, first, count)
                 if first + count == BLOCKS:
                     to_multiply.extend([(r, i) for i in range(BLOCKS)])
             to_quantise = []
 
-            for n in range(SPAN):
+            for n in range(STEP_BLOCKS):
                 if n < len(units(k + 1)):
                     y_to_features(*units(k + 1)[n])
-                if n < len(units(k - 1)):
-                    corr_to_tokens(k - 1, n)
-            for n in range(min(len(to_multiply), PASSES_A_STEP, ready) if units(k) else len(to_multiply)):
-                r, i = to_multiply.pop(0)
+                if n < len(units(k - CORRECT_LAG)):
+                    corr_to_tokens(k - CORRECT_LAG, n)
+            passes = min(PASSES_A_STEP, ready) if units(k) else len(to_multiply)
+            for r, i in to_multiply[:passes]:
                 multiply(r, i)
                 if r == ROUNDS - 1:
                     store_block(PARTS - 1, i)
                 elif (r + 1) % PASSES == 0:
                     to_store.append((k + COPY_LAG, r // PASSES, i))
+            to_multiply = to_multiply[passes:]

from contextlib import ExitStack

import concourse.mybir as mybir
from concourse.masks import make_identity

F32 = mybir.dt.float32
BF16 = mybir.dt.bfloat16
U32 = mybir.dt.uint32
U8 = mybir.dt.uint8
E4M3_X4 = mybir.dt.float8_e4m3fn_x4
E5M2_X4 = mybir.dt.float8_e5m2_x4
FUNC = mybir.ActivationFunctionType
ALU = mybir.AluOpType

P = 128
PACK = 4
K_PASS = P * PACK
TOKENS = 4096
PARTS = 2
D = 512
PASSES = TOKENS // K_PASS
BLOCKS = D // P
VEC_ROWS = PARTS * BLOCKS
ROUNDS = PARTS * PASSES
BANK = PACK * P

STEP_BLOCKS = 2
STEPS_A_ROUND = BLOCKS // STEP_BLOCKS
X_CHUNK = STEP_BLOCKS * P

CORRECT_LAG = 1
FINISH_LAG = 2
PASSES_A_STEP = 2
COPY_LAG = 2
LOAD_LEAD = 3
DAMP_SCALAR_COLS = 192
X_VECTOR = 96
X_FILL = 3

FLOPS = 2 * PARTS * TOKENS * D * D


def tile_better_transformer_t_v_kernel(
    tc, x, weights, bias, gain, norm_bias, gamma, beta, y, grad_out, out
):
    nc = tc.nc
    x_view = x.rearrange("(c p j) f -> c p j f", p=P, j=PACK)
    y_view = y.rearrange("(c p j) f -> c p j f", p=P, j=PACK)
    g_view = grad_out.rearrange("(c p j) f -> c p j f", p=P, j=PACK)

    with ExitStack() as ctx:
        consts = ctx.enter_context(tc.tile_pool(name="consts", bufs=1))
        loads = ctx.enter_context(tc.tile_pool(name="loads", bufs=6))
        work = ctx.enter_context(tc.tile_pool(name="work", bufs=3))
        grouped = ctx.enter_context(tc.tile_pool(name="grouped", bufs=4))
        quant = ctx.enter_context(tc.tile_pool(name="quant", bufs=6))
        results = ctx.enter_context(tc.tile_pool(name="results", bufs=BLOCKS))
        acc_pool = ctx.enter_context(tc.psum_pool(name="acc", bufs=1))
        to_features = ctx.enter_context(tc.psum_pool(name="to_features", bufs=2))
        to_tokens = ctx.enter_context(tc.psum_pool(name="to_tokens", bufs=2))
        ctx.enter_context(tc.manual_schedule())

        steps = []
        for r in range(ROUNDS):
            for b in range(0, BLOCKS, STEP_BLOCKS):
                steps.append([(r, b + n) for n in range(STEP_BLOCKS)])
        last_units = steps.pop()
        steps.extend([u] for u in last_units)

        def units(k):
            return steps[k] if 0 <= k < len(steps) else []

        x_raw, y_raw, g_raw = {}, {}, {}
        x_grouped, x_codes, x_scales = {}, {}, {}
        dy_grouped, dy_codes, dy_scales = {}, {}, {}
        y_t, corr_t = {}, {}
        tanh_half, silu, damped, corr = {}, {}, {}, {}
        acc = {}

        def block_cols(b):
            return slice(b * P, (b + 1) * P)

        def const_col(r, b):
            col = r // PASSES * BLOCKS + b
            return slice(col, col + 1)

        def load(raw, view, dtype, name, bufs, r, lo, width):
            part, c = divmod(r, PASSES)
            if lo == 0:
                raw[r] = loads.tile([P, PACK, D], dtype, name=name, bufs=bufs)
            nc.sync.dma_start(
                out=raw[r][:, :, lo : lo + width],
                in_=view[c, :, :, part * D + lo : part * D + lo + width],
            )

        def load_x(r):
            load(x_raw, x_view, BF16, "x_raw", 6, r, 0, D)

        def load_y(r, lo=0, width=D):
            load(y_raw, y_view, F32, "y_raw", 6, r, lo, width)

        def load_g(r):
            load(g_raw, g_view, BF16, "g_raw", 8, r, 0, D)

        def x_norm(q, vector_cols):
            r, half = divmod(q, STEPS_A_ROUND)
            if half == 0:
                x_grouped[r] = grouped.tile([P, D, PACK], BF16, name="x_grouped", align_bytes=64)
            lo = half * X_CHUNK
            cut = lo + vector_cols
            hi = lo + X_CHUNK
            nc.vector.tensor_scalar(
                out=x_grouped[r][:, lo:cut, :].rearrange("p (n i) j -> p n j i", i=4),
                in0=x_raw[r][:, :, lo:cut].rearrange("p j (n i) -> p n j i", i=4),
                scalar1=gain_col[:, 0:1], scalar2=shift_col[:, 0:1],
                op0=ALU.mult, op1=ALU.add,
            )
            if cut < hi:
                nc.scalar.activation(
                    out=x_grouped[r][:, cut:hi, :].rearrange("p (n i) j -> p n j i", i=4),
                    in_=x_raw[r][:, :, cut:hi].rearrange("p j (n i) -> p n j i", i=4),
                    func=FUNC.Identity,
                    bias=shift_col[:, 0:1],
                    scale=gain_col[:, 0:1],
                )

        def quantise(src, codes, scales, dtype, name, r, first, count):
            if first == 0:
                codes[r] = quant.tile([P, D], U32, name=name + "_codes", align_bytes=64)
                scales[r] = quant.tile([P, D], U8, name=name + "_scales", align_bytes=64)
            cols = slice(first * P, (first + count) * P)
            nc.vector.quantize_mx(
                out=codes[r][:, cols].bitcast(dtype),
                scales=scales[r][:, cols],
                in_=src[r][:, cols, :].rearrange("p w j -> p (w j)"),
            )

        def quantise_x(r):
            quantise(x_grouped, x_codes, x_scales, E4M3_X4, "x", r, 0, BLOCKS)

        def quantise_dy(r, first, count):
            quantise(dy_grouped, dy_codes, dy_scales, E5M2_X4, "dy", r, first, count)

        def y_to_features(r, b):
            y_t[r, b] = to_features.tile([P, PACK, P], F32, name="y_t")
            for j in range(PACK):
                nc.tensor.transpose(y_t[r, b][:, j, :], y_raw[r][:, j, block_cols(b)], ident[:])

        def step_tile(k, name, bufs):
            return work.tile([P, len(steps[k]) * BANK], F32, name=name, bufs=bufs)

        def unit_cols(n):
            return slice(n * BANK, (n + 1) * BANK)

        def activations(k):
            for tiles, name, func, scale_col in (
                (tanh_half, "tanh_half", FUNC.Tanh, half_beta_col),
                (silu, "silu", FUNC.Silu, beta_col),
            ):
                tiles[k] = step_tile(k, name, 3)
                for n, (r, b) in enumerate(steps[k]):
                    nc.scalar.activation(
                        out=tiles[k][:, unit_cols(n)],
                        in_=y_t[r, b][:].rearrange("p j f -> p (j f)"),
                        func=func, scale=scale_col[:, const_col(r, b)],
                    )

        def damp(k):
            damped[k] = step_tile(k, "damped", 2)
            scalar_cols = DAMP_SCALAR_COLS * len(steps[k]) // STEP_BLOCKS
            for n, (r, b) in enumerate(steps[k]):
                lo, hi = unit_cols(n).start, unit_cols(n).stop
                cut = hi - scalar_cols if n == len(steps[k]) - 1 else hi
                scale, shift = damp_col[:, const_col(r, b)], neg_damp_col[:, const_col(r, b)]
                nc.gpsimd.tensor_scalar(
                    out=damped[k][:, lo:cut], in0=tanh_half[k][:, lo:cut],
                    scalar1=scale, scalar2=shift, op0=ALU.mult, op1=ALU.add,
                )
                if cut < hi:
                    nc.scalar.activation(
                        out=damped[k][:, cut:hi], in_=tanh_half[k][:, cut:hi],
                        func=FUNC.Identity, scale=scale, bias=shift,
                    )

        def correct(k):
            corr[k] = step_tile(k, "corr", 3)
            nc.vector.scalar_tensor_tensor(
                out=corr[k][:], in0=silu[k][:], scalar=1.0, in1=damped[k][:],
                op0=ALU.subtract, op1=ALU.mult,
            )

        def corr_to_tokens(k, n):
            r, b = steps[k][n]
            corr_t[r, b] = to_tokens.tile([P, PACK, P], F32, name="corr_t")
            for j in range(PACK):
                lo = unit_cols(n).start + j * P
                nc.tensor.transpose(corr_t[r, b][:, j, :], corr[k][:, lo : lo + P], ident[:])

        def finish_dy(r, b):
            if b == 0:
                dy_grouped[r] = grouped.tile([P, D, PACK], BF16, name="dy_grouped", align_bytes=64)
            nc.vector.scalar_tensor_tensor(
                out=dy_grouped[r][:, block_cols(b), :],
                in0=corr_t[r, b][:].rearrange("p j f -> p f j"),
                scalar=1.0,
                in1=g_raw[r][:, :, block_cols(b)].rearrange("p j f -> p f j"),
                op0=ALU.add, op1=ALU.mult,
            )

        def multiply(r, i):
            part, c = divmod(r, PASSES)
            if c == 0:
                acc[part, i] = acc_pool.tile([P, D], F32, name="acc%d" % i)
            nc.tensor.matmul_mx(
                out=acc[part, i][:],
                lhsT=x_codes[r][:, block_cols(i)].bitcast(E4M3_X4),
                lhsT_scale=x_scales[r][:, block_cols(i)],
                rhs=dy_codes[r][:].bitcast(E5M2_X4),
                rhs_scale=dy_scales[r][:],
                start=(c == 0),
                stop=(c == PASSES - 1),
            )

        def store_block(part, i):
            result = results.tile([P, D], F32, name="result")
            if i % 2 == 0 and part == PARTS - 1:
                nc.vector.tensor_copy(out=result[:], in_=acc[part, i][:])
            else:
                nc.scalar.copy(out=result[:], in_=acc[part, i][:])
            nc.sync.dma_start(out=out[part, i * P : (i + 1) * P, :], in_=result[:])

        table_in = consts.tile([P, 1], F32)
        nc.vector.memset(table_in[:], 0.0)
        table_out = consts.tile([P, 1], F32)
        nc.scalar.activation(out=table_out[:], in_=table_in[:], func=FUNC.Silu)

        ident = consts.tile([P, P], F32)
        make_identity(nc, ident[:])

        gain_bf = consts.tile([P, 1], BF16)
        nc.sync.dma_start(out=gain_bf[:], in_=gain.partition_broadcast(P))
        shift_bf = consts.tile([P, 1], BF16)
        nc.sync.dma_start(out=shift_bf[:], in_=norm_bias.partition_broadcast(P))
        vec_bf = consts.tile([2 * VEC_ROWS, P], BF16)
        nc.sync.dma_start(out=vec_bf[0:VEC_ROWS, :], in_=beta.rearrange("(r f) -> r f", f=P))
        nc.sync.dma_start(
            out=vec_bf[VEC_ROWS : 2 * VEC_ROWS, :], in_=gamma.rearrange("(r f) -> r f", f=P)
        )
        load_y(0, 0, P)
        load_y(0, P, P)
        load_x(0)
        load_y(0, 2 * P, 2 * P)
        load_g(0)
        load_y(1, 0, 2 * P)
        load_x(1)
        load_y(1, 2 * P, 2 * P)
        load_g(1)
        load_y(2)
        load_x(2)
        load_g(2)

        gain_col = consts.tile([P, 1], F32)
        nc.vector.tensor_copy(out=gain_col[:], in_=gain_bf[:])
        shift_col = consts.tile([P, 1], F32)
        nc.vector.tensor_copy(out=shift_col[:], in_=shift_bf[:])
        vec_rows = consts.tile([P, P], F32)
        nc.vector.memset(vec_rows[:], 0.0)
        nc.vector.tensor_copy(out=vec_rows[0 : 2 * VEC_ROWS, :], in_=vec_bf[:])
        vec_cols = to_features.tile([P, P], F32, tag="y_t")
        nc.tensor.transpose(vec_cols[:], vec_rows[:], ident[:])
        beta_col = consts.tile([P, VEC_ROWS], F32)
        nc.vector.tensor_copy(out=beta_col[:], in_=vec_cols[:, 0:VEC_ROWS])
        half_beta_col = consts.tile([P, VEC_ROWS], F32)
        nc.vector.tensor_scalar_mul(out=half_beta_col[:], in0=vec_cols[:, 0:VEC_ROWS], scalar1=0.5)
        damp_col = consts.tile([P, VEC_ROWS], F32)
        nc.vector.tensor_scalar(
            out=damp_col[:], in0=vec_cols[:, VEC_ROWS : 2 * VEC_ROWS],
            scalar1=1.0, scalar2=0.5, op0=ALU.subtract, op1=ALU.mult,
        )

        neg_damp_col = consts.tile([P, VEC_ROWS], F32)
        nc.vector.tensor_scalar(
            out=neg_damp_col[:], in0=vec_cols[:, VEC_ROWS : 2 * VEC_ROWS],
            scalar1=-0.5, scalar2=0.5, op0=ALU.mult, op1=ALU.add,
        )

        for u in units(0):
            y_to_features(*u)

        to_quantise = []
        to_multiply = []
        to_store = []
        for k in range(len(steps) + FINISH_LAG):
            ready = len(to_multiply)
            starts_round = k % STEPS_A_ROUND == 0
            if starts_round and k // STEPS_A_ROUND + LOAD_LEAD < ROUNDS:
                load_y(k // STEPS_A_ROUND + LOAD_LEAD)
                load_x(k // STEPS_A_ROUND + LOAD_LEAD)
                load_g(k // STEPS_A_ROUND + LOAD_LEAD)

            while to_store and to_store[0][0] <= k:
                store_block(*to_store.pop(0)[1:])
            if units(k):
                activations(k)

            if units(k - CORRECT_LAG):
                correct(k - CORRECT_LAG)
            if units(k):
                damp(k)
            for r, b in units(k - FINISH_LAG):
                finish_dy(r, b)
                if r < ROUNDS - 1 and b == BLOCKS - 1:
                    to_quantise.append((r, 0, BLOCKS))
                elif r == ROUNDS - 1 and b % STEP_BLOCKS == 1 and b < BLOCKS - 1:
                    to_quantise.append((r, b - 1, STEP_BLOCKS))
                elif r == ROUNDS - 1 and b >= BLOCKS - STEP_BLOCKS:
                    to_quantise.append((r, b, 1))
            if k < ROUNDS * STEPS_A_ROUND:
                x_norm(k, X_CHUNK if k < X_FILL or to_store else X_VECTOR)
            if starts_round and 0 < k <= ROUNDS * STEPS_A_ROUND:
                quantise_x(k // STEPS_A_ROUND - 1)
            for r, first, count in to_quantise:
                quantise_dy(r, first, count)
                if first + count == BLOCKS:
                    to_multiply.extend([(r, i) for i in range(BLOCKS)])
            to_quantise = []

            for n in range(STEP_BLOCKS):
                if n < len(units(k + 1)):
                    y_to_features(*units(k + 1)[n])
                if n < len(units(k - CORRECT_LAG)):
                    corr_to_tokens(k - CORRECT_LAG, n)
            passes = min(PASSES_A_STEP, ready) if units(k) else len(to_multiply)
            for r, i in to_multiply[:passes]:
                multiply(r, i)
                if r == ROUNDS - 1:
                    store_block(PARTS - 1, i)
                elif (r + 1) % PASSES == 0:
                    to_store.append((k + COPY_LAG, r // PASSES, i))
            to_multiply = to_multiply[passes:]
